import numpy as np
import ml_dtypes


def mxq(x, axis, fmt="e4m3"):
    dtype, down = {"e4m3": (ml_dtypes.float8_e4m3fn, 7), "e5m2": (ml_dtypes.float8_e5m2, 14)}[fmt]
    v = np.moveaxis(np.asarray(x, np.float32).astype(ml_dtypes.bfloat16).astype(np.float64), axis, -1)
    blocks = v.reshape(v.shape[:-1] + (-1, 32))
    amax = np.abs(blocks).max(-1, keepdims=True)
    byte = np.maximum(np.where(amax > 0, np.frexp(amax)[1] - 1 + 127, 0) - down, 1)
    scale = np.exp2(byte - 127.0)
    codes = (blocks / scale).astype(np.float32).astype(dtype).astype(np.float64)
    return np.moveaxis((codes * scale).reshape(v.shape), -1, axis)


WIDE = False


def mx_kscale(k):
    if not WIDE:
        return np.ones(k)
    levels = np.array([10, -10, 5, -5, 0])
    a = np.random.permutation(np.resize(levels, k // 512 * 4)).reshape(k // 512, 4)
    idx = np.arange(k)
    return np.exp2(a[idx // 512, idx % 128 // 32])


BF16 = ml_dtypes.bfloat16


def bf(x):
    return np.asarray(x, np.float32).astype(BF16)


def f64(x):
    return np.asarray(x).astype(np.float64)


E2M1 = np.array([0.0, 0.5, 1.0, 1.5, 2.0, 3.0, 4.0, 6.0, -0.0, -0.5, -1.0, -1.5, -2.0, -3.0, -4.0, -6.0])


def pack_weight(w, fmt):
    k, n = w.shape
    w = f64(bf(w)).reshape(k // 32, 32, n)
    amax = np.abs(w).max(1)
    if fmt == "e4m3":
        byte = np.frexp(amax)[1] - 1 + 127 - 7
    else:
        mant, ex = np.frexp(amax / 6.0)
        byte = np.where(mant > 0.5, ex, ex - 1) + 127
    byte = np.clip(np.where(amax > 0, byte, 1), 1, 254)
    scaled = (w * np.exp2(127.0 - byte)[:, None, :]).reshape(k, n).astype(np.float32)
    by_word = np.ascontiguousarray(scaled.reshape(k // 512, 128, 4, n).transpose(0, 1, 3, 2))
    if fmt == "e4m3":
        words = by_word.astype(ml_dtypes.float8_e4m3fn).view(np.uint8)
    else:
        c = by_word.astype(ml_dtypes.float4_e2m1fn).view(np.uint8) & 0xF
        words = c[..., 0::2] | (c[..., 1::2] << 4)
    return np.ascontiguousarray(words), np.ascontiguousarray(byte.astype(np.uint8).reshape(k // 512, 16, n))


def unpack_weight(words, scales, fmt):
    g, p, n, _ = words.shape
    if fmt == "e4m3":
        vals = np.ascontiguousarray(words).view(ml_dtypes.float8_e4m3fn).astype(np.float64)
    else:
        nib = np.empty((g, p, n, 4), np.uint8)
        nib[..., 0::2] = words & 0xF
        nib[..., 1::2] = words >> 4
        vals = E2M1[nib]
    vals = vals * np.repeat(np.exp2(scales.astype(np.float64) - 127.0), 8, axis=1)[..., None]
    return vals.transpose(0, 1, 3, 2).reshape(g * 512, n)

def pack4(w):
    words, scales = pack_weight(w, "e2m1")
    return words.reshape(words.shape[0], 128, -1), scales


def unpack4(words, scales):
    return unpack_weight(words.reshape(words.shape[0], 128, -1, 2), scales, "e2m1")


S, D = 4096, 1024
HALF = D // 2
BASE = 10000.0


def rope_interleaved(v):
    freqs = 1.0 / BASE ** (np.arange(HALF) / HALF)
    ang = np.arange(S)[:, None] * freqs[None, :]
    cos, sin = np.cos(ang), np.sin(ang)
    vp = v.reshape(S, HALF, 2)
    vr, vi = vp[..., 0], vp[..., 1]
    rot = np.stack([vr * cos - vi * sin, vr * sin + vi * cos], axis=-1)
    return rot.reshape(S, D)


def setup_inputs():
    s = mx_kscale(D)
    x = bf(np.random.standard_normal((S, D)) * s)
    w = np.random.standard_normal((D, D)) / np.sqrt(D) / s[None, :]
    words, scales = pack4(np.ascontiguousarray(w.T))
    return {"x": x, "w_words": words, "w_scales": scales}


def reference(x, w_words, w_scales):
    y = mxq(f64(x), 1, "e4m3") @ unpack4(w_words, w_scales)
    return rope_interleaved(y)

@@ -1,0 +1,185 @@
+import math
+from contextlib import ExitStack
+
+import concourse.mybir as mybir
+from concourse.masks import make_identity
+
+F32 = mybir.dt.float32
+BF16 = mybir.dt.bfloat16
+I32 = mybir.dt.int32
+U32 = mybir.dt.uint32
+U8 = mybir.dt.uint8
+FP8X4 = mybir.dt.float8_e4m3fn_x4
+FP4X4 = mybir.dt.float4_e2m1fn_x4
+ALU = mybir.AluOpType
+ACT = mybir.ActivationFunctionType
+
+S = 4096
+D = 1024
+P = 128
+PACK = 4
+K_PASS = P * PACK
+PASSES = D // K_PASS
+BANK = 512
+BANKS_OUT = D // BANK
+PAIRS = D // 2
+BANK_PAIRS = BANK // 2
+TILES = S // P
+LOAD_TILES = 4
+STORE_TILES = 2
+BASE = 10000.0
+DIGIT = 8
+
+FLOPS = 2 * S * D * D
+
+
+def build_turns_per_token(nc, turns):
+    digits = turns.rearrange("p (a b c) -> p a b c", a=DIGIT, b=DIGIT)
+    step = BASE ** (-1.0 / PAIRS)
+    nc.vector.memset(turns, 1.0)
+    for a in range(DIGIT):
+        part = digits[:, a, :, :]
+        nc.scalar.mul(out=part, in_=part, mul=step ** (DIGIT * DIGIT * a) / (2.0 * math.pi))
+    for b in range(1, DIGIT):
+        part = digits[:, :, b, :]
+        nc.scalar.mul(out=part, in_=part, mul=step ** (DIGIT * b))
+    for c in range(1, DIGIT):
+        part = digits[:, :, :, c]
+        nc.scalar.mul(out=part, in_=part, mul=step**c)
+
+
+def tile_ropeattention_pa_t_kernel(tc, x, w_words, w_scales, out):
+    nc = tc.nc
+    x_tiles = x.rearrange("(p t) k -> p t k", t=TILES)
+    out_tiles = out.rearrange("(p t) n -> p t n", t=TILES)
+
+    with ExitStack() as stack:
+        const = stack.enter_context(tc.tile_pool(name="const", bufs=1))
+        x_pool = stack.enter_context(tc.tile_pool(name="x", bufs=TILES // LOAD_TILES))
+        quant = stack.enter_context(tc.tile_pool(name="quant", bufs=3))
+        trig = stack.enter_context(tc.tile_pool(name="trig", bufs=3))
+        rot = stack.enter_context(tc.tile_pool(name="rot", bufs=3))
+        psum_t = stack.enter_context(tc.psum_pool(name="psum_t", bufs=2))
+        psum_y = stack.enter_context(tc.psum_pool(name="psum_y", bufs=6))
+
+        x_chunks = []
+        for c in range(TILES // LOAD_TILES):
+            x_chunk = x_pool.tile([P, LOAD_TILES, D], BF16, name="x_chunk")
+            x_chunks.append(x_chunk)
+
+        def load_x(c):
+            nc.sync.dma_start(
+                out=x_chunks[c][:], in_=x_tiles[:, c * LOAD_TILES : (c + 1) * LOAD_TILES, :]
+            )
+
+        load_x(0)
+
+        w_planes = const.tile([P, PASSES, D], U8, align_bytes=64)
+        nc.vector.memset(w_planes[:].bitcast(I32), 0)
+        for q in range(4):
+            nc.sync.dma_start(
+                out=w_planes[32 * q : 32 * q + 4, :, :].bitcast(I32),
+                in_=w_scales[:, 4 * q : 4 * q + 4, :].rearrange("g r n -> r g n").bitcast(I32),
+            )
+        w_codes = const.tile([P, PASSES, 2 * D], U8, align_bytes=64)
+        for g in range(PASSES):
+            nc.sync.dma_start(out=w_codes[:, g, :].bitcast(I32), in_=w_words[g].bitcast(I32))
+        for c in range(1, TILES // LOAD_TILES):
+            load_x(c)
+
+        ident = const.tile([P, P], F32)
+        make_identity(nc, ident[:])
+        position_int = const.tile([P, TILES], I32)
+        nc.gpsimd.iota(out=position_int[:], pattern=[[1, TILES]], base=0, channel_multiplier=TILES)
+        position = const.tile([P, TILES], F32)
+        nc.vector.tensor_copy(out=position[:], in_=position_int[:])
+        turns = const.tile([P, PAIRS], F32)
+        build_turns_per_token(nc, turns[:])
+
+        for t in range(TILES):
+            x_words = x_chunks[t // LOAD_TILES][:, t % LOAD_TILES, :].bitcast(F32)
+            flipped = psum_t.tile([P, PASSES, 2, P], F32)
+            for g in range(PASSES):
+                for u in range(2):
+                    nc.tensor.transpose(
+                        flipped[:, g, u, :],
+                        x_words[:, 256 * g + u : 256 * (g + 1) : 2],
+                        ident[:],
+                    )
+            grouped = quant.tile([P, PASSES, P, PACK], BF16, align_bytes=64)
+            nc.scalar.copy(
+                out=grouped[:].bitcast(F32), in_=flipped[:].rearrange("p g u r -> p g r u")
+            )
+            x_codes = quant.tile([P, PASSES * P], U32, align_bytes=64)
+            x_planes = quant.tile([P, PASSES * P], U8, align_bytes=64)
+            nc.vector.quantize_mx(
+                out=x_codes[:].bitcast(FP8X4),
+                scales=x_planes[:],
+                in_=grouped[:].rearrange("p g r j -> p (g r j)"),
+            )
+
+            place = position[:, t : t + 1]
+            whole = trig.tile([P, PAIRS], U32)
+            nc.scalar.activation(out=whole[:], in_=turns[:], func=ACT.Copy, scale=place)
+            frac = trig.tile([P, PAIRS], F32)
+            nc.vector.scalar_tensor_tensor(
+                out=frac[:],
+                in0=turns[:],
+                scalar=place,
+                in1=whole[:].bitcast(I32),
+                op0=ALU.mult,
+                op1=ALU.subtract,
+            )
+            sine = trig.tile([P, PAIRS], F32)
+            nc.scalar.activation(out=sine[:], in_=frac[:], func=ACT.Sin, scale=2.0 * math.pi)
+            half_sine = trig.tile([P, PAIRS], F32)
+            nc.scalar.activation(out=half_sine[:], in_=frac[:], func=ACT.Sin, scale=math.pi)
+            versine = trig.tile([P, PAIRS], F32)
+            nc.scalar.activation(
+                out=versine[:], in_=half_sine[:], func=ACT.Square, scale=math.sqrt(2.0)
+            )
+
+            if t % STORE_TILES == 0:
+                result = rot.tile([P, STORE_TILES, D], F32)
+            rotated = result[:, t % STORE_TILES, :].rearrange("p (i e) -> p i e", e=2)
+            crossed = rot.tile([P, 2, PAIRS], F32)
+            for h in range(BANKS_OUT):
+                y = psum_y.tile([P, BANK], F32)
+                for g in range(PASSES):
+                    nc.tensor.matmul_mx(
+                        out=y[:],
+                        lhsT=x_codes[:, g * P : (g + 1) * P].bitcast(FP8X4),
+                        lhsT_scale=x_planes[:, g * P : (g + 1) * P],
+                        rhs=w_codes[:, g, 2 * BANK * h : 2 * BANK * (h + 1)].bitcast(FP4X4),
+                        rhs_scale=w_planes[:, g, BANK * h : BANK * (h + 1)],
+                        start=(g == 0),
+                        stop=(g == PASSES - 1),
+                    )
+                pairs = slice(BANK_PAIRS * h, BANK_PAIRS * (h + 1))
+                y_pairs = y[:].rearrange("p (i e) -> p i e", e=2)
+                nc.vector.scalar_tensor_tensor(
+                    out=rotated[:, pairs, :],
+                    in0=versine[:, pairs].unsqueeze(2).to_broadcast([P, BANK_PAIRS, 2]),
+                    scalar=1.0,
+                    in1=y_pairs,
+                    op0=ALU.subtract,
+                    op1=ALU.mult,
+                )
+                nc.vector.scalar_tensor_tensor(
+                    out=crossed[:, 0, pairs],
+                    in0=y_pairs[:, :, 1],
+                    scalar=-1.0,
+                    in1=sine[:, pairs],
+                    op0=ALU.mult,
+                    op1=ALU.mult,
+                )
+                nc.vector.tensor_tensor(
+                    out=crossed[:, 1, pairs], in0=y_pairs[:, :, 0], in1=sine[:, pairs], op=ALU.mult
+                )
+            nc.gpsimd.tensor_tensor(
+                out=rotated, in0=crossed[:].rearrange("p e i -> p i e"), in1=rotated, op=ALU.subtract
+            )
+            if t % STORE_TILES == STORE_TILES - 1:
+                nc.sync.dma_start(
+                    out=out_tiles[:, t + 1 - STORE_TILES : t + 1, :], in_=result[:]
+                )

@@ -25,10 +25,16 @@ BANKS_OUT = D // BANK
 PAIRS = D // 2
 BANK_PAIRS = BANK // 2
 TILES = S // P
-LOAD_TILES = 4
-STORE_TILES = 2
+CHUNK = 4
+CHUNKS = TILES // CHUNK
+TILE_WORDS = PASSES * P
 BASE = 10000.0
 DIGIT = 8
+
+FLIP_AHEAD = CHUNK + 1
+WHOLE_AHEAD = 2
+TRIG_AHEAD = 1
+PROJECT_AHEAD = 1
 
 FLOPS = 2 * S * D * D
 
@@ -54,26 +60,25 @@ def tile_ropeattention_pa_t_kernel(tc, x, w_words, w_scales, out):
     out_tiles = out.rearrange("(p t) n -> p t n", t=TILES)
 
     with ExitStack() as stack:
+        stack.enter_context(tc.manual_schedule())
         const = stack.enter_context(tc.tile_pool(name="const", bufs=1))
-        x_pool = stack.enter_context(tc.tile_pool(name="x", bufs=TILES // LOAD_TILES))
-        quant = stack.enter_context(tc.tile_pool(name="quant", bufs=3))
+        x_pool = stack.enter_context(tc.tile_pool(name="x", bufs=CHUNKS))
+        quant = stack.enter_context(tc.tile_pool(name="quant", bufs=2))
         trig = stack.enter_context(tc.tile_pool(name="trig", bufs=3))
-        rot = stack.enter_context(tc.tile_pool(name="rot", bufs=3))
-        psum_t = stack.enter_context(tc.psum_pool(name="psum_t", bufs=2))
-        psum_y = stack.enter_context(tc.psum_pool(name="psum_y", bufs=6))
+        rot = stack.enter_context(tc.tile_pool(name="rot", bufs=4))
+        psum_c = stack.enter_context(tc.psum_pool(name="psum_c", bufs=1))
+        psum_t = stack.enter_context(tc.psum_pool(name="psum_t", bufs=3))
+        psum_y = stack.enter_context(tc.psum_pool(name="psum_y", bufs=2 * BANKS_OUT))
 
         x_chunks = []
-        for c in range(TILES // LOAD_TILES):
-            x_chunk = x_pool.tile([P, LOAD_TILES, D], BF16, name="x_chunk")
+        for c in range(CHUNKS):
+            x_chunk = x_pool.tile([P, CHUNK, D], BF16)
             x_chunks.append(x_chunk)
 
         def load_x(c):
-            nc.sync.dma_start(
-                out=x_chunks[c][:], in_=x_tiles[:, c * LOAD_TILES : (c + 1) * LOAD_TILES, :]
-            )
+            nc.sync.dma_start(out=x_chunks[c][:], in_=x_tiles[:, c * CHUNK : (c + 1) * CHUNK, :])
 
         load_x(0)
-
         w_planes = const.tile([P, PASSES, D], U8, align_bytes=64)
         nc.vector.memset(w_planes[:].bitcast(I32), 0)
         for q in range(4):
@@ -84,7 +89,7 @@ def tile_ropeattention_pa_t_kernel(tc, x, w_words, w_scales, out):
         w_codes = const.tile([P, PASSES, 2 * D], U8, align_bytes=64)
         for g in range(PASSES):
             nc.sync.dma_start(out=w_codes[:, g, :].bitcast(I32), in_=w_words[g].bitcast(I32))
-        for c in range(1, TILES // LOAD_TILES):
+        for c in range(1, CHUNKS):
             load_x(c)
 
         ident = const.tile([P, P], F32)
@@ -95,54 +100,86 @@ def tile_ropeattention_pa_t_kernel(tc, x, w_words, w_scales, out):
         nc.vector.tensor_copy(out=position[:], in_=position_int[:])
         turns = const.tile([P, PAIRS], F32)
         build_turns_per_token(nc, turns[:])
+        turns_flipped = psum_t.tile([P, PAIRS // P, P], F32, tag="flipped")
+        for b in range(PAIRS // P):
+            nc.tensor.transpose(turns_flipped[:, b, :], turns[:, b * P : (b + 1) * P], ident[:])
+        turns_columns = const.tile([P, PAIRS // P, P], F32)
+        nc.scalar.copy(out=turns_columns[:], in_=turns_flipped[:])
+        turns_psum = psum_c.tile([P, PAIRS], F32)
+        for b in range(PAIRS // P):
+            nc.tensor.transpose(turns_psum[:, b * P : (b + 1) * P], turns_columns[:, b, :], ident[:])
 
-        for t in range(TILES):
-            x_words = x_chunks[t // LOAD_TILES][:, t % LOAD_TILES, :].bitcast(F32)
+        grouped_of = {}
+        x_codes_of = {}
+        x_planes_of = {}
+        whole_of = {}
+        frac_of = {}
+        sine_of = {}
+        versine_of = {}
+        y_of = {}
+
+        def flip(t):
+            x_words = x_chunks[t // CHUNK][:, t % CHUNK, :].bitcast(F32)
             flipped = psum_t.tile([P, PASSES, 2, P], F32)
             for g in range(PASSES):
                 for u in range(2):
                     nc.tensor.transpose(
-                        flipped[:, g, u, :],
-                        x_words[:, 256 * g + u : 256 * (g + 1) : 2],
-                        ident[:],
+                        flipped[:, g, u, :], x_words[:, 256 * g + u : 256 * (g + 1) : 2], ident[:]
                     )
-            grouped = quant.tile([P, PASSES, P, PACK], BF16, align_bytes=64)
+            if t % CHUNK == 0:
+                grouped = quant.tile([P, CHUNK, PASSES, P, PACK], BF16, align_bytes=64)
+                grouped_of[t // CHUNK] = grouped
             nc.scalar.copy(
-                out=grouped[:].bitcast(F32), in_=flipped[:].rearrange("p g u r -> p g r u")
+                out=grouped_of[t // CHUNK][:, t % CHUNK].bitcast(F32),
+                in_=flipped[:].rearrange("p g u r -> p g r u"),
             )
-            x_codes = quant.tile([P, PASSES * P], U32, align_bytes=64)
-            x_planes = quant.tile([P, PASSES * P], U8, align_bytes=64)
+
+        def quantise(c):
+            x_codes = quant.tile([P, CHUNK * TILE_WORDS], U32, align_bytes=64)
+            x_planes = quant.tile([P, CHUNK * TILE_WORDS], U8, align_bytes=64)
             nc.vector.quantize_mx(
                 out=x_codes[:].bitcast(FP8X4),
                 scales=x_planes[:],
-                in_=grouped[:].rearrange("p g r j -> p (g r j)"),
+                in_=grouped_of[c][:].rearrange("p t g r j -> p (t g r j)"),
             )
+            x_codes_of[c] = x_codes
+            x_planes_of[c] = x_planes
 
-            place = position[:, t : t + 1]
+        def whole_turns(t):
             whole = trig.tile([P, PAIRS], U32)
-            nc.scalar.activation(out=whole[:], in_=turns[:], func=ACT.Copy, scale=place)
+            nc.scalar.activation(
+                out=whole[:], in_=turns[:], func=ACT.Copy, scale=position[:, t : t + 1]
+            )
+            whole_of[t] = whole
+
+        def fraction(t):
             frac = trig.tile([P, PAIRS], F32)
             nc.vector.scalar_tensor_tensor(
                 out=frac[:],
-                in0=turns[:],
-                scalar=place,
-                in1=whole[:].bitcast(I32),
+                in0=turns_psum[:],
+                scalar=position[:, t : t + 1],
+                in1=whole_of[t][:].bitcast(I32),
                 op0=ALU.mult,
                 op1=ALU.subtract,
             )
-            sine = trig.tile([P, PAIRS], F32)
-            nc.scalar.activation(out=sine[:], in_=frac[:], func=ACT.Sin, scale=2.0 * math.pi)
+            frac_of[t] = frac
+
+        def sine_and_versine(t):
             half_sine = trig.tile([P, PAIRS], F32)
-            nc.scalar.activation(out=half_sine[:], in_=frac[:], func=ACT.Sin, scale=math.pi)
+            nc.scalar.activation(out=half_sine[:], in_=frac_of[t][:], func=ACT.Sin, scale=math.pi)
+            sine = trig.tile([P, PAIRS], F32)
+            nc.scalar.activation(out=sine[:], in_=frac_of[t][:], func=ACT.Sin, scale=2.0 * math.pi)
             versine = trig.tile([P, PAIRS], F32)
             nc.scalar.activation(
                 out=versine[:], in_=half_sine[:], func=ACT.Square, scale=math.sqrt(2.0)
             )
+            sine_of[t] = sine
+            versine_of[t] = versine
 
-            if t % STORE_TILES == 0:
-                result = rot.tile([P, STORE_TILES, D], F32)
-            rotated = result[:, t % STORE_TILES, :].rearrange("p (i e) -> p i e", e=2)
-            crossed = rot.tile([P, 2, PAIRS], F32)
+        def project(t):
+            words = slice((t % CHUNK) * TILE_WORDS, (t % CHUNK + 1) * TILE_WORDS)
+            x_codes = x_codes_of[t // CHUNK][:, words]
+            x_planes = x_planes_of[t // CHUNK][:, words]
             for h in range(BANKS_OUT):
                 y = psum_y.tile([P, BANK], F32)
                 for g in range(PASSES):
@@ -155,11 +192,18 @@ def tile_ropeattention_pa_t_kernel(tc, x, w_words, w_scales, out):
                         start=(g == 0),
                         stop=(g == PASSES - 1),
                     )
+                y_of[(t, h)] = y
+
+        def rotate_and_store(t):
+            result = rot.tile([P, PAIRS, 2], F32)
+            crossed = rot.tile([P, 2, PAIRS], F32)
+            for h in range(BANKS_OUT):
                 pairs = slice(BANK_PAIRS * h, BANK_PAIRS * (h + 1))
-                y_pairs = y[:].rearrange("p (i e) -> p i e", e=2)
+                y_pairs = y_of[(t, h)][:].rearrange("p (i e) -> p i e", e=2)
+                sine = sine_of[t][:, pairs]
                 nc.vector.scalar_tensor_tensor(
-                    out=rotated[:, pairs, :],
-                    in0=versine[:, pairs].unsqueeze(2).to_broadcast([P, BANK_PAIRS, 2]),
+                    out=result[:, pairs, :],
+                    in0=versine_of[t][:, pairs].unsqueeze(2).to_broadcast([P, BANK_PAIRS, 2]),
                     scalar=1.0,
                     in1=y_pairs,
                     op0=ALU.subtract,
@@ -169,17 +213,35 @@ def tile_ropeattention_pa_t_kernel(tc, x, w_words, w_scales, out):
                     out=crossed[:, 0, pairs],
                     in0=y_pairs[:, :, 1],
                     scalar=-1.0,
-                    in1=sine[:, pairs],
+                    in1=sine,
                     op0=ALU.mult,
                     op1=ALU.mult,
                 )
                 nc.vector.tensor_tensor(
-                    out=crossed[:, 1, pairs], in0=y_pairs[:, :, 0], in1=sine[:, pairs], op=ALU.mult
+                    out=crossed[:, 1, pairs], in0=y_pairs[:, :, 0], in1=sine, op=ALU.mult
                 )
-            nc.gpsimd.tensor_tensor(
-                out=rotated, in0=crossed[:].rearrange("p e i -> p i e"), in1=rotated, op=ALU.subtract
-            )
-            if t % STORE_TILES == STORE_TILES - 1:
-                nc.sync.dma_start(
-                    out=out_tiles[:, t + 1 - STORE_TILES : t + 1, :], in_=result[:]
+                nc.gpsimd.tensor_tensor(
+                    out=result[:, pairs, :],
+                    in0=crossed[:, :, pairs].rearrange("p e i -> p i e"),
+                    in1=result[:, pairs, :],
+                    op=ALU.subtract,
                 )
+            nc.sync.dma_start(out=out_tiles[:, t, :], in_=result[:].rearrange("p i e -> p (i e)"))
+
+        def in_range(t):
+            return 0 <= t < TILES
+
+        for t in range(-FLIP_AHEAD, TILES):
+            if in_range(t + FLIP_AHEAD):
+                flip(t + FLIP_AHEAD)
+            if in_range(t + WHOLE_AHEAD):
+                whole_turns(t + WHOLE_AHEAD)
+            if in_range(t + TRIG_AHEAD):
+                sine_and_versine(t + TRIG_AHEAD)
+                project(t + PROJECT_AHEAD)
+            if in_range(t):
+                rotate_and_store(t)
+            if in_range(t + WHOLE_AHEAD):
+                fraction(t + WHOLE_AHEAD)
+            if in_range(t + FLIP_AHEAD) and (t + FLIP_AHEAD) % CHUNK == CHUNK - 1:
+                quantise((t + FLIP_AHEAD) // CHUNK)

@@ -30,6 +30,8 @@ CHUNKS = TILES // CHUNK
 TILE_WORDS = PASSES * P
 BASE = 10000.0
 DIGIT = 8
+SLOW = 400
+assert (S - 1) * BASE ** (-SLOW / PAIRS) < math.pi
 
 FLIP_AHEAD = CHUNK + 1
 WHOLE_AHEAD = 2
@@ -45,13 +47,15 @@ def build_turns_per_token(nc, turns):
     nc.vector.memset(turns, 1.0)
     for a in range(DIGIT):
         part = digits[:, a, :, :]
-        nc.scalar.mul(out=part, in_=part, mul=step ** (DIGIT * DIGIT * a) / (2.0 * math.pi))
+        nc.vector.tensor_scalar_mul(
+            out=part, in0=part, scalar1=step ** (DIGIT * DIGIT * a) / (2.0 * math.pi)
+        )
     for b in range(1, DIGIT):
         part = digits[:, :, b, :]
-        nc.scalar.mul(out=part, in_=part, mul=step ** (DIGIT * b))
+        nc.vector.tensor_scalar_mul(out=part, in0=part, scalar1=step ** (DIGIT * b))
     for c in range(1, DIGIT):
         part = digits[:, :, :, c]
-        nc.scalar.mul(out=part, in_=part, mul=step**c)
+        nc.vector.tensor_scalar_mul(out=part, in0=part, scalar1=step**c)
 
 
 def tile_ropeattention_pa_t_kernel(tc, x, w_words, w_scales, out):
@@ -67,8 +71,8 @@ def tile_ropeattention_pa_t_kernel(tc, x, w_words, w_scales, out):
         trig = stack.enter_context(tc.tile_pool(name="trig", bufs=3))
         rot = stack.enter_context(tc.tile_pool(name="rot", bufs=4))
         psum_c = stack.enter_context(tc.psum_pool(name="psum_c", bufs=1))
-        psum_t = stack.enter_context(tc.psum_pool(name="psum_t", bufs=3))
-        psum_y = stack.enter_context(tc.psum_pool(name="psum_y", bufs=2 * BANKS_OUT))
+        psum_t = stack.enter_context(tc.psum_pool(name="psum_t", bufs=2))
+        psum_y = stack.enter_context(tc.psum_pool(name="psum_y", bufs=5))
 
         x_chunks = []
         for c in range(CHUNKS):
@@ -92,14 +96,14 @@ def tile_ropeattention_pa_t_kernel(tc, x, w_words, w_scales, out):
         for c in range(1, CHUNKS):
             load_x(c)
 
+        turns = const.tile([P, PAIRS], F32)
+        build_turns_per_token(nc, turns[:])
         ident = const.tile([P, P], F32)
         make_identity(nc, ident[:])
         position_int = const.tile([P, TILES], I32)
         nc.gpsimd.iota(out=position_int[:], pattern=[[1, TILES]], base=0, channel_multiplier=TILES)
         position = const.tile([P, TILES], F32)
         nc.vector.tensor_copy(out=position[:], in_=position_int[:])
-        turns = const.tile([P, PAIRS], F32)
-        build_turns_per_token(nc, turns[:])
         turns_flipped = psum_t.tile([P, PAIRS // P, P], F32, tag="flipped")
         for b in range(PAIRS // P):
             nc.tensor.transpose(turns_flipped[:, b, :], turns[:, b * P : (b + 1) * P], ident[:])
@@ -146,23 +150,23 @@ def tile_ropeattention_pa_t_kernel(tc, x, w_words, w_scales, out):
             x_planes_of[c] = x_planes
 
         def whole_turns(t):
-            whole = trig.tile([P, PAIRS], U32)
-            nc.scalar.activation(
-                out=whole[:], in_=turns[:], func=ACT.Copy, scale=position[:, t : t + 1]
-            )
+            place = position[:, t : t + 1]
+            whole = trig.tile([P, SLOW], U32)
+            nc.scalar.activation(out=whole[:], in_=turns[:, :SLOW], func=ACT.Copy, scale=place)
+            frac = trig.tile([P, PAIRS], F32)
+            nc.scalar.activation(out=frac[:, SLOW:], in_=turns[:, SLOW:], func=ACT.Copy, scale=place)
             whole_of[t] = whole
+            frac_of[t] = frac
 
         def fraction(t):
-            frac = trig.tile([P, PAIRS], F32)
             nc.vector.scalar_tensor_tensor(
-                out=frac[:],
-                in0=turns_psum[:],
+                out=frac_of[t][:, :SLOW],
+                in0=turns_psum[:, :SLOW],
                 scalar=position[:, t : t + 1],
                 in1=whole_of[t][:].bitcast(I32),
                 op0=ALU.mult,
                 op1=ALU.subtract,
             )
-            frac_of[t] = frac
 
         def sine_and_versine(t):
             half_sine = trig.tile([P, PAIRS], F32)
@@ -226,7 +230,10 @@ def tile_ropeattention_pa_t_kernel(tc, x, w_words, w_scales, out):
                     in1=result[:, pairs, :],
                     op=ALU.subtract,
                 )
-            nc.sync.dma_start(out=out_tiles[:, t, :], in_=result[:].rearrange("p i e -> p (i e)"))
+                nc.sync.dma_start(
+                    out=out_tiles[:, t, BANK * h : BANK * (h + 1)],
+                    in_=result[:, pairs, :].rearrange("p i e -> p (i e)"),
+                )
 
         def in_range(t):
             return 0 <= t < TILES

@@ -26,17 +26,21 @@ PAIRS = D // 2
 BANK_PAIRS = BANK // 2
 TILES = S // P
 CHUNK = 4
-CHUNKS = TILES // CHUNK
+CHUNK_TILES = (1, 1, 2) + (CHUNK,) * 7
+assert sum(CHUNK_TILES) == TILES
+CHUNKS = len(CHUNK_TILES)
+CHUNK_FIRST = tuple(sum(CHUNK_TILES[:c]) for c in range(CHUNKS))
 TILE_WORDS = PASSES * P
 BASE = 10000.0
 DIGIT = 8
 SLOW = 400
 assert (S - 1) * BASE ** (-SLOW / PAIRS) < math.pi
 
-FLIP_AHEAD = CHUNK + 1
 WHOLE_AHEAD = 2
 TRIG_AHEAD = 1
 PROJECT_AHEAD = 1
+FIRST_STEP = -2
+EARLY_TILES = 2
 
 FLOPS = 2 * S * D * D
 
@@ -58,6 +62,16 @@ def build_turns_per_token(nc, turns):
         nc.vector.tensor_scalar_mul(out=part, in0=part, scalar1=step**c)
 
 
+def flips_by_step():
+    plan = {FIRST_STEP: list(range(CHUNK_TILES[0]))}
+    for c in range(1, CHUNKS):
+        steps = CHUNK_TILES[c - 1]
+        a_step = -(-CHUNK_TILES[c] // steps)
+        for j in range(CHUNK_TILES[c]):
+            plan.setdefault(CHUNK_FIRST[c] - 1 - steps + j // a_step, []).append(CHUNK_FIRST[c] + j)
+    return plan
+
+
 def tile_ropeattention_pa_t_kernel(tc, x, w_words, w_scales, out):
     nc = tc.nc
     x_tiles = x.rearrange("(p t) k -> p t k", t=TILES)
@@ -66,23 +80,26 @@ def tile_ropeattention_pa_t_kernel(tc, x, w_words, w_scales, out):
     with ExitStack() as stack:
         stack.enter_context(tc.manual_schedule())
         const = stack.enter_context(tc.tile_pool(name="const", bufs=1))
-        x_pool = stack.enter_context(tc.tile_pool(name="x", bufs=CHUNKS))
-        quant = stack.enter_context(tc.tile_pool(name="quant", bufs=2))
-        trig = stack.enter_context(tc.tile_pool(name="trig", bufs=3))
-        rot = stack.enter_context(tc.tile_pool(name="rot", bufs=4))
+        quant = stack.enter_context(tc.tile_pool(name="quant", bufs=3))
+        trig = stack.enter_context(tc.tile_pool(name="trig", bufs=4))
+        rot = stack.enter_context(tc.tile_pool(name="rot", bufs=6))
         psum_c = stack.enter_context(tc.psum_pool(name="psum_c", bufs=1))
         psum_t = stack.enter_context(tc.psum_pool(name="psum_t", bufs=2))
         psum_y = stack.enter_context(tc.psum_pool(name="psum_y", bufs=5))
 
-        x_chunks = []
-        for c in range(CHUNKS):
-            x_chunk = x_pool.tile([P, CHUNK, D], BF16)
-            x_chunks.append(x_chunk)
+        zero = const.tile([P, 1], F32)
+        nc.gpsimd.memset(zero[:], 0.0)
+        unused = const.tile([P, 1], F32)
+        nc.scalar.activation(out=unused[:], in_=zero[:], func=ACT.Sin)
+
+        x_all = const.tile([P, TILES, D], BF16)
 
         def load_x(c):
-            nc.sync.dma_start(out=x_chunks[c][:], in_=x_tiles[:, c * CHUNK : (c + 1) * CHUNK, :])
+            tiles = slice(CHUNK_FIRST[c], CHUNK_FIRST[c] + CHUNK_TILES[c])
+            nc.sync.dma_start(out=x_all[:, tiles, :], in_=x_tiles[:, tiles, :])
 
         load_x(0)
+        load_x(1)
         w_planes = const.tile([P, PASSES, D], U8, align_bytes=64)
         nc.vector.memset(w_planes[:].bitcast(I32), 0)
         for q in range(4):
@@ -93,7 +110,7 @@ def tile_ropeattention_pa_t_kernel(tc, x, w_words, w_scales, out):
         w_codes = const.tile([P, PASSES, 2 * D], U8, align_bytes=64)
         for g in range(PASSES):
             nc.sync.dma_start(out=w_codes[:, g, :].bitcast(I32), in_=w_words[g].bitcast(I32))
-        for c in range(1, CHUNKS):
+        for c in range(2, CHUNKS):
             load_x(c)
 
         turns = const.tile([P, PAIRS], F32)
@@ -104,15 +121,25 @@ def tile_ropeattention_pa_t_kernel(tc, x, w_words, w_scales, out):
         nc.gpsimd.iota(out=position_int[:], pattern=[[1, TILES]], base=0, channel_multiplier=TILES)
         position = const.tile([P, TILES], F32)
         nc.vector.tensor_copy(out=position[:], in_=position_int[:])
-        turns_flipped = psum_t.tile([P, PAIRS // P, P], F32, tag="flipped")
-        for b in range(PAIRS // P):
-            nc.tensor.transpose(turns_flipped[:, b, :], turns[:, b * P : (b + 1) * P], ident[:])
         turns_columns = const.tile([P, PAIRS // P, P], F32)
-        nc.scalar.copy(out=turns_columns[:], in_=turns_flipped[:])
         turns_psum = psum_c.tile([P, PAIRS], F32)
-        for b in range(PAIRS // P):
-            nc.tensor.transpose(turns_psum[:, b * P : (b + 1) * P], turns_columns[:, b, :], ident[:])
 
+        def turns_to_columns():
+            turns_flipped = psum_t.tile([P, PAIRS // P, P], F32, tag="flipped")
+            for b in range(PAIRS // P):
+                nc.tensor.transpose(turns_flipped[:, b, :], turns[:, b * P : (b + 1) * P], ident[:])
+            nc.vector.tensor_copy(out=turns_columns[:], in_=turns_flipped[:])
+
+        def columns_to_psum():
+            for b in range(PAIRS // P):
+                nc.tensor.transpose(
+                    turns_psum[:, b * P : (b + 1) * P], turns_columns[:, b, :], ident[:]
+                )
+
+        chunk_of = {}
+        for c in range(CHUNKS):
+            for j in range(CHUNK_TILES[c]):
+                chunk_of[CHUNK_FIRST[c] + j] = c
         grouped_of = {}
         x_codes_of = {}
         x_planes_of = {}
@@ -121,30 +148,34 @@ def tile_ropeattention_pa_t_kernel(tc, x, w_words, w_scales, out):
         sine_of = {}
         versine_of = {}
         y_of = {}
+        result_of = {}
+        crossed_of = {}
 
         def flip(t):
-            x_words = x_chunks[t // CHUNK][:, t % CHUNK, :].bitcast(F32)
+            c = chunk_of[t]
+            x_words = x_all[:, t, :].bitcast(F32)
             flipped = psum_t.tile([P, PASSES, 2, P], F32)
             for g in range(PASSES):
                 for u in range(2):
                     nc.tensor.transpose(
                         flipped[:, g, u, :], x_words[:, 256 * g + u : 256 * (g + 1) : 2], ident[:]
                     )
-            if t % CHUNK == 0:
+            if t == CHUNK_FIRST[c]:
                 grouped = quant.tile([P, CHUNK, PASSES, P, PACK], BF16, align_bytes=64)
-                grouped_of[t // CHUNK] = grouped
+                grouped_of[c] = grouped
             nc.scalar.copy(
-                out=grouped_of[t // CHUNK][:, t % CHUNK].bitcast(F32),
+                out=grouped_of[c][:, t - CHUNK_FIRST[c]].bitcast(F32),
                 in_=flipped[:].rearrange("p g u r -> p g r u"),
             )
 
         def quantise(c):
+            words = CHUNK_TILES[c] * TILE_WORDS
             x_codes = quant.tile([P, CHUNK * TILE_WORDS], U32, align_bytes=64)
             x_planes = quant.tile([P, CHUNK * TILE_WORDS], U8, align_bytes=64)
             nc.vector.quantize_mx(
-                out=x_codes[:].bitcast(FP8X4),
-                scales=x_planes[:],
-                in_=grouped_of[c][:].rearrange("p t g r j -> p (t g r j)"),
+                out=x_codes[:, :words].bitcast(FP8X4),
+                scales=x_planes[:, :words],
+                in_=grouped_of[c][:, : CHUNK_TILES[c]].rearrange("p t g r j -> p (t g r j)"),
             )
             x_codes_of[c] = x_codes
             x_planes_of[c] = x_planes
@@ -161,7 +192,7 @@ def tile_ropeattention_pa_t_kernel(tc, x, w_words, w_scales, out):
         def fraction(t):
             nc.vector.scalar_tensor_tensor(
                 out=frac_of[t][:, :SLOW],
-                in0=turns_psum[:, :SLOW],
+                in0=(turns if t < EARLY_TILES else turns_psum)[:, :SLOW],
                 scalar=position[:, t : t + 1],
                 in1=whole_of[t][:].bitcast(I32),
                 op0=ALU.mult,
@@ -181,9 +212,10 @@ def tile_ropeattention_pa_t_kernel(tc, x, w_words, w_scales, out):
             versine_of[t] = versine
 
         def project(t):
-            words = slice((t % CHUNK) * TILE_WORDS, (t % CHUNK + 1) * TILE_WORDS)
-            x_codes = x_codes_of[t // CHUNK][:, words]
-            x_planes = x_planes_of[t // CHUNK][:, words]
+            c = chunk_of[t]
+            first_word = (t - CHUNK_FIRST[c]) * TILE_WORDS
+            x_codes = x_codes_of[c][:, first_word : first_word + TILE_WORDS]
+            x_planes = x_planes_of[c][:, first_word : first_word + TILE_WORDS]
             for h in range(BANKS_OUT):
                 y = psum_y.tile([P, BANK], F32)
                 for g in range(PASSES):
@@ -198,57 +230,69 @@ def tile_ropeattention_pa_t_kernel(tc, x, w_words, w_scales, out):
                     )
                 y_of[(t, h)] = y
 
-        def rotate_and_store(t):
-            result = rot.tile([P, PAIRS, 2], F32)
-            crossed = rot.tile([P, 2, PAIRS], F32)
-            for h in range(BANKS_OUT):
-                pairs = slice(BANK_PAIRS * h, BANK_PAIRS * (h + 1))
-                y_pairs = y_of[(t, h)][:].rearrange("p (i e) -> p i e", e=2)
-                sine = sine_of[t][:, pairs]
-                nc.vector.scalar_tensor_tensor(
-                    out=result[:, pairs, :],
-                    in0=versine_of[t][:, pairs].unsqueeze(2).to_broadcast([P, BANK_PAIRS, 2]),
-                    scalar=1.0,
-                    in1=y_pairs,
-                    op0=ALU.subtract,
-                    op1=ALU.mult,
-                )
-                nc.vector.scalar_tensor_tensor(
-                    out=crossed[:, 0, pairs],
-                    in0=y_pairs[:, :, 1],
-                    scalar=-1.0,
-                    in1=sine,
-                    op0=ALU.mult,
-                    op1=ALU.mult,
-                )
-                nc.vector.tensor_tensor(
-                    out=crossed[:, 1, pairs], in0=y_pairs[:, :, 0], in1=sine, op=ALU.mult
-                )
-                nc.gpsimd.tensor_tensor(
-                    out=result[:, pairs, :],
-                    in0=crossed[:, :, pairs].rearrange("p e i -> p i e"),
-                    in1=result[:, pairs, :],
-                    op=ALU.subtract,
-                )
-                nc.sync.dma_start(
-                    out=out_tiles[:, t, BANK * h : BANK * (h + 1)],
-                    in_=result[:, pairs, :].rearrange("p i e -> p (i e)"),
-                )
+        def rotate_and_store(t, h):
+            if h == 0:
+                result = rot.tile([P, PAIRS, 2], F32)
+                crossed = rot.tile([P, 2, PAIRS], F32)
+                result_of[t] = result
+                crossed_of[t] = crossed
+            result = result_of[t]
+            crossed = crossed_of[t]
+            pairs = slice(BANK_PAIRS * h, BANK_PAIRS * (h + 1))
+            y_pairs = y_of[(t, h)][:].rearrange("p (i e) -> p i e", e=2)
+            sine = sine_of[t][:, pairs]
+            nc.vector.scalar_tensor_tensor(
+                out=result[:, pairs, :],
+                in0=versine_of[t][:, pairs].unsqueeze(2).to_broadcast([P, BANK_PAIRS, 2]),
+                scalar=1.0,
+                in1=y_pairs,
+                op0=ALU.subtract,
+                op1=ALU.mult,
+            )
+            nc.vector.scalar_tensor_tensor(
+                out=crossed[:, 0, pairs],
+                in0=y_pairs[:, :, 1],
+                scalar=-1.0,
+                in1=sine,
+                op0=ALU.mult,
+                op1=ALU.mult,
+            )
+            nc.vector.tensor_tensor(
+                out=crossed[:, 1, pairs], in0=y_pairs[:, :, 0], in1=sine, op=ALU.mult
+            )
+            nc.gpsimd.tensor_tensor(
+                out=result[:, pairs, :],
+                in0=crossed[:, :, pairs].rearrange("p e i -> p i e"),
+                in1=result[:, pairs, :],
+                op=ALU.subtract,
+            )
+            nc.sync.dma_start(
+                out=out_tiles[:, t, BANK * h : BANK * (h + 1)],
+                in_=result[:, pairs, :].rearrange("p i e -> p (i e)"),
+            )
 
         def in_range(t):
             return 0 <= t < TILES
 
-        for t in range(-FLIP_AHEAD, TILES):
-            if in_range(t + FLIP_AHEAD):
-                flip(t + FLIP_AHEAD)
-            if in_range(t + WHOLE_AHEAD):
-                whole_turns(t + WHOLE_AHEAD)
+        flips_in = flips_by_step()
+        for t in range(FIRST_STEP, TILES):
             if in_range(t + TRIG_AHEAD):
                 sine_and_versine(t + TRIG_AHEAD)
-                project(t + PROJECT_AHEAD)
+            if in_range(t + WHOLE_AHEAD):
+                whole_turns(t + WHOLE_AHEAD)
+            for flipped_tile in flips_in.get(t, []):
+                flip(flipped_tile)
+            if t == FIRST_STEP + 1:
+                turns_to_columns()
             if in_range(t):
-                rotate_and_store(t)
+                rotate_and_store(t, 0)
+            if t + PROJECT_AHEAD in CHUNK_FIRST:
+                quantise(chunk_of[t + PROJECT_AHEAD])
+            if in_range(t + PROJECT_AHEAD):
+                project(t + PROJECT_AHEAD)
+            if t == FIRST_STEP + 1:
+                columns_to_psum()
+            if in_range(t):
+                rotate_and_store(t, 1)
             if in_range(t + WHOLE_AHEAD):
                 fraction(t + WHOLE_AHEAD)
-            if in_range(t + FLIP_AHEAD) and (t + FLIP_AHEAD) % CHUNK == CHUNK - 1:
-                quantise((t + FLIP_AHEAD) // CHUNK)

@@ -260,7 +260,8 @@ def tile_ropeattention_pa_t_kernel(tc, x, w_words, w_scales, out):
             nc.vector.tensor_tensor(
                 out=crossed[:, 1, pairs], in0=y_pairs[:, :, 0], in1=sine, op=ALU.mult
             )
-            nc.gpsimd.tensor_tensor(
+            subtractor = nc.vector if (t, h) == (TILES - 1, BANKS_OUT - 1) else nc.gpsimd
+            subtractor.tensor_tensor(
                 out=result[:, pairs, :],
                 in0=crossed[:, :, pairs].rearrange("p e i -> p i e"),
                 in1=result[:, pairs, :],
@@ -282,12 +283,12 @@ def tile_ropeattention_pa_t_kernel(tc, x, w_words, w_scales, out):
                 whole_turns(t + WHOLE_AHEAD)
             for flipped_tile in flips_in.get(t, []):
                 flip(flipped_tile)
-            if t == FIRST_STEP + 1:
-                turns_to_columns()
             if in_range(t):
                 rotate_and_store(t, 0)
             if t + PROJECT_AHEAD in CHUNK_FIRST:
                 quantise(chunk_of[t + PROJECT_AHEAD])
+            if t == FIRST_STEP + 1:
+                turns_to_columns()
             if in_range(t + PROJECT_AHEAD):
                 project(t + PROJECT_AHEAD)
             if t == FIRST_STEP + 1:

@@ -33,8 +33,12 @@ CHUNK_FIRST = tuple(sum(CHUNK_TILES[:c]) for c in range(CHUNKS))
 TILE_WORDS = PASSES * P
 BASE = 10000.0
 DIGIT = 8
-SLOW = 400
-assert (S - 1) * BASE ** (-SLOW / PAIRS) < math.pi
+
+
+def fast_pairs(t):
+    last_token = P * t + P - 1
+    return min(i for i in range(PAIRS) if last_token * BASE ** (-i / PAIRS) < math.pi)
+
 
 WHOLE_AHEAD = 2
 TRIG_AHEAD = 1
@@ -74,8 +78,8 @@ def flips_by_step():
 
 def tile_ropeattention_pa_t_kernel(tc, x, w_words, w_scales, out):
     nc = tc.nc
-    x_tiles = x.rearrange("(p t) k -> p t k", t=TILES)
-    out_tiles = out.rearrange("(p t) n -> p t n", t=TILES)
+    x_tiles = x.rearrange("(t p) k -> p t k", p=P)
+    out_tiles = out.rearrange("(t p) n -> p t n", p=P)
 
     with ExitStack() as stack:
         stack.enter_context(tc.manual_schedule())
@@ -118,9 +122,13 @@ def tile_ropeattention_pa_t_kernel(tc, x, w_words, w_scales, out):
         ident = const.tile([P, P], F32)
         make_identity(nc, ident[:])
         position_int = const.tile([P, TILES], I32)
-        nc.gpsimd.iota(out=position_int[:], pattern=[[1, TILES]], base=0, channel_multiplier=TILES)
+        nc.gpsimd.iota(out=position_int[:], pattern=[[P, TILES]], base=0, channel_multiplier=1)
         position = const.tile([P, TILES], F32)
         nc.vector.tensor_copy(out=position[:], in_=position_int[:])
+        half_turn = const.tile([P, TILES], F32)
+        nc.vector.tensor_scalar_mul(out=half_turn[:], in0=position[:], scalar1=math.pi)
+        full_turn = const.tile([P, TILES], F32)
+        nc.vector.tensor_scalar_mul(out=full_turn[:], in0=position[:], scalar1=2.0 * math.pi)
         turns_columns = const.tile([P, PAIRS // P, P], F32)
         turns_psum = psum_c.tile([P, PAIRS], F32)
 
@@ -181,29 +189,42 @@ def tile_ropeattention_pa_t_kernel(tc, x, w_words, w_scales, out):
             x_planes_of[c] = x_planes
 
         def whole_turns(t):
-            place = position[:, t : t + 1]
-            whole = trig.tile([P, SLOW], U32)
-            nc.scalar.activation(out=whole[:], in_=turns[:, :SLOW], func=ACT.Copy, scale=place)
-            frac = trig.tile([P, PAIRS], F32)
-            nc.scalar.activation(out=frac[:, SLOW:], in_=turns[:, SLOW:], func=ACT.Copy, scale=place)
+            fast = fast_pairs(t)
+            whole = trig.tile([P, PAIRS], U32)
+            nc.scalar.activation(
+                out=whole[:, :fast], in_=turns[:, :fast], func=ACT.Copy, scale=position[:, t : t + 1]
+            )
             whole_of[t] = whole
-            frac_of[t] = frac
 
         def fraction(t):
+            fast = fast_pairs(t)
+            frac = trig.tile([P, PAIRS], F32)
             nc.vector.scalar_tensor_tensor(
-                out=frac_of[t][:, :SLOW],
-                in0=(turns if t < EARLY_TILES else turns_psum)[:, :SLOW],
+                out=frac[:, :fast],
+                in0=(turns if t < EARLY_TILES else turns_psum)[:, :fast],
                 scalar=position[:, t : t + 1],
-                in1=whole_of[t][:].bitcast(I32),
+                in1=whole_of[t][:, :fast].bitcast(I32),
                 op0=ALU.mult,
                 op1=ALU.subtract,
             )
+            frac_of[t] = frac
 
         def sine_and_versine(t):
+            fast = fast_pairs(t)
             half_sine = trig.tile([P, PAIRS], F32)
-            nc.scalar.activation(out=half_sine[:], in_=frac_of[t][:], func=ACT.Sin, scale=math.pi)
             sine = trig.tile([P, PAIRS], F32)
-            nc.scalar.activation(out=sine[:], in_=frac_of[t][:], func=ACT.Sin, scale=2.0 * math.pi)
+            nc.scalar.activation(
+                out=half_sine[:, fast:], in_=turns[:, fast:], func=ACT.Sin, scale=half_turn[:, t : t + 1]
+            )
+            nc.scalar.activation(
+                out=sine[:, fast:], in_=turns[:, fast:], func=ACT.Sin, scale=full_turn[:, t : t + 1]
+            )
+            nc.scalar.activation(
+                out=half_sine[:, :fast], in_=frac_of[t][:, :fast], func=ACT.Sin, scale=math.pi
+            )
+            nc.scalar.activation(
+                out=sine[:, :fast], in_=frac_of[t][:, :fast], func=ACT.Sin, scale=2.0 * math.pi
+            )
             versine = trig.tile([P, PAIRS], F32)
             nc.scalar.activation(
                 out=versine[:], in_=half_sine[:], func=ACT.Square, scale=math.sqrt(2.0)

@@ -25,6 +25,7 @@ BANKS_OUT = D // BANK
 PAIRS = D // 2
 BANK_PAIRS = BANK // 2
 TILES = S // P
+GROUP = 4
 CHUNK = 4
 CHUNK_TILES = (1, 1, 2) + (CHUNK,) * 7
 assert sum(CHUNK_TILES) == TILES
@@ -36,7 +37,7 @@ DIGIT = 8
 
 
 def fast_pairs(t):
-    last_token = P * t + P - 1
+    last_token = GROUP * P * (t // GROUP) + GROUP * (P - 1) + t % GROUP
     return min(i for i in range(PAIRS) if last_token * BASE ** (-i / PAIRS) < math.pi)
 
 
@@ -78,8 +79,8 @@ def flips_by_step():
 
 def tile_ropeattention_pa_t_kernel(tc, x, w_words, w_scales, out):
     nc = tc.nc
-    x_tiles = x.rearrange("(t p) k -> p t k", p=P)
-    out_tiles = out.rearrange("(t p) n -> p t n", p=P)
+    x_groups = x.rearrange("(c p j) k -> p c j k", p=P, j=GROUP)
+    out_groups = out.rearrange("(c p j) n -> p c j n", p=P, j=GROUP)
 
     with ExitStack() as stack:
         stack.enter_context(tc.manual_schedule())
@@ -99,8 +100,12 @@ def tile_ropeattention_pa_t_kernel(tc, x, w_words, w_scales, out):
         x_all = const.tile([P, TILES, D], BF16)
 
         def load_x(c):
-            tiles = slice(CHUNK_FIRST[c], CHUNK_FIRST[c] + CHUNK_TILES[c])
-            nc.sync.dma_start(out=x_all[:, tiles, :], in_=x_tiles[:, tiles, :])
+            first = CHUNK_FIRST[c]
+            count = CHUNK_TILES[c]
+            nc.sync.dma_start(
+                out=x_all[:, first : first + count, :],
+                in_=x_groups[:, first // GROUP, first % GROUP : first % GROUP + count, :],
+            )
 
         load_x(0)
         load_x(1)
@@ -122,7 +127,12 @@ def tile_ropeattention_pa_t_kernel(tc, x, w_words, w_scales, out):
         ident = const.tile([P, P], F32)
         make_identity(nc, ident[:])
         position_int = const.tile([P, TILES], I32)
-        nc.gpsimd.iota(out=position_int[:], pattern=[[P, TILES]], base=0, channel_multiplier=1)
+        nc.gpsimd.iota(
+            out=position_int[:],
+            pattern=[[GROUP * P, TILES // GROUP], [1, GROUP]],
+            base=0,
+            channel_multiplier=GROUP,
+        )
         position = const.tile([P, TILES], F32)
         nc.vector.tensor_copy(out=position[:], in_=position_int[:])
         half_turn = const.tile([P, TILES], F32)
@@ -289,7 +299,7 @@ def tile_ropeattention_pa_t_kernel(tc, x, w_words, w_scales, out):
                 op=ALU.subtract,
             )
             nc.sync.dma_start(
-                out=out_tiles[:, t, BANK * h : BANK * (h + 1)],
+                out=out_groups[:, t // GROUP, t % GROUP, BANK * h : BANK * (h + 1)],
                 in_=result[:, pairs, :].rearrange("p i e -> p (i e)"),
             )
 

@@ -87,10 +87,11 @@ def tile_ropeattention_pa_t_kernel(tc, x, w_words, w_scales, out):
         const = stack.enter_context(tc.tile_pool(name="const", bufs=1))
         quant = stack.enter_context(tc.tile_pool(name="quant", bufs=3))
         trig = stack.enter_context(tc.tile_pool(name="trig", bufs=4))
-        rot = stack.enter_context(tc.tile_pool(name="rot", bufs=6))
+        rot = stack.enter_context(tc.tile_pool(name="rot", bufs=8))
         psum_c = stack.enter_context(tc.psum_pool(name="psum_c", bufs=1))
         psum_t = stack.enter_context(tc.psum_pool(name="psum_t", bufs=2))
-        psum_y = stack.enter_context(tc.psum_pool(name="psum_y", bufs=5))
+        psum_y = stack.enter_context(tc.psum_pool(name="psum_y", bufs=4))
+        psum_s = stack.enter_context(tc.psum_pool(name="psum_s", bufs=1))
 
         zero = const.tile([P, 1], F32)
         nc.gpsimd.memset(zero[:], 0.0)
@@ -126,6 +127,8 @@ def tile_ropeattention_pa_t_kernel(tc, x, w_words, w_scales, out):
         build_turns_per_token(nc, turns[:])
         ident = const.tile([P, P], F32)
         make_identity(nc, ident[:])
+        minus_ident = const.tile([P, P], F32)
+        nc.vector.tensor_scalar_mul(out=minus_ident[:], in0=ident[:], scalar1=-1.0)
         position_int = const.tile([P, TILES], I32)
         nc.gpsimd.iota(
             out=position_int[:],
@@ -291,6 +294,8 @@ def tile_ropeattention_pa_t_kernel(tc, x, w_words, w_scales, out):
             nc.vector.tensor_tensor(
                 out=crossed[:, 1, pairs], in0=y_pairs[:, :, 0], in1=sine, op=ALU.mult
             )
+            if tensor_subtracts(t, h):
+                return
             subtractor = nc.vector if (t, h) == (TILES - 1, BANKS_OUT - 1) else nc.gpsimd
             subtractor.tensor_tensor(
                 out=result[:, pairs, :],
@@ -298,22 +303,59 @@ def tile_ropeattention_pa_t_kernel(tc, x, w_words, w_scales, out):
                 in1=result[:, pairs, :],
                 op=ALU.subtract,
             )
+            store(t, h)
+
+        def store(t, h):
+            pairs = slice(BANK_PAIRS * h, BANK_PAIRS * (h + 1))
             nc.sync.dma_start(
                 out=out_groups[:, t // GROUP, t % GROUP, BANK * h : BANK * (h + 1)],
-                in_=result[:, pairs, :].rearrange("p i e -> p (i e)"),
+                in_=result_of[t][:, pairs, :].rearrange("p i e -> p (i e)"),
             )
+
+        def tensor_subtracts(t, h):
+            return h == 0 and t % CHUNK == CHUNK - 2
+
+        difference_of = {}
+
+        def subtract_on_tensor(t, h):
+            pairs = slice(BANK_PAIRS * h, BANK_PAIRS * (h + 1))
+            difference = psum_s.tile([P, BANK_PAIRS, 2], F32)
+            nc.tensor.matmul(
+                out=difference[:],
+                lhsT=ident[:],
+                rhs=crossed_of[t][:, :, pairs].rearrange("p e i -> p i e"),
+                start=True,
+                stop=False,
+            )
+            nc.tensor.matmul(
+                out=difference[:],
+                lhsT=minus_ident[:],
+                rhs=result_of[t][:, pairs, :],
+                start=False,
+                stop=True,
+            )
+            difference_of[(t, h)] = difference
+
+        def copy_difference_and_store(t, h):
+            pairs = slice(BANK_PAIRS * h, BANK_PAIRS * (h + 1))
+            nc.scalar.copy(out=result_of[t][:, pairs, :], in_=difference_of[(t, h)][:])
+            store(t, h)
 
         def in_range(t):
             return 0 <= t < TILES
 
         flips_in = flips_by_step()
         for t in range(FIRST_STEP, TILES):
+            if in_range(t - 1) and tensor_subtracts(t - 1, 0):
+                subtract_on_tensor(t - 1, 0)
             if in_range(t + TRIG_AHEAD):
                 sine_and_versine(t + TRIG_AHEAD)
             if in_range(t + WHOLE_AHEAD):
                 whole_turns(t + WHOLE_AHEAD)
             for flipped_tile in flips_in.get(t, []):
                 flip(flipped_tile)
+            if in_range(t - 1) and tensor_subtracts(t - 1, 0):
+                copy_difference_and_store(t - 1, 0)
             if in_range(t):
                 rotate_and_store(t, 0)
             if t + PROJECT_AHEAD in CHUNK_FIRST:

@@ -38,7 +38,7 @@ DIGIT = 8
 
 def fast_pairs(t):
     last_token = GROUP * P * (t // GROUP) + GROUP * (P - 1) + t % GROUP
-    return min(i for i in range(PAIRS) if last_token * BASE ** (-i / PAIRS) < math.pi)
+    return min(i for i in range(PAIRS) if last_token * BASE ** (-i / PAIRS) < 2.0 * math.pi)
 
 
 WHOLE_AHEAD = 2
@@ -205,7 +205,11 @@ def tile_ropeattention_pa_t_kernel(tc, x, w_words, w_scales, out):
             fast = fast_pairs(t)
             whole = trig.tile([P, PAIRS], U32)
             nc.scalar.activation(
-                out=whole[:, :fast], in_=turns[:, :fast], func=ACT.Copy, scale=position[:, t : t + 1]
+                out=whole[:, :fast],
+                in_=turns[:, :fast],
+                func=ACT.Copy,
+                scale=position[:, t : t + 1],
+                bias=-0.5,
             )
             whole_of[t] = whole
 
@@ -230,13 +234,21 @@ def tile_ropeattention_pa_t_kernel(tc, x, w_words, w_scales, out):
                 out=half_sine[:, fast:], in_=turns[:, fast:], func=ACT.Sin, scale=half_turn[:, t : t + 1]
             )
             nc.scalar.activation(
-                out=sine[:, fast:], in_=turns[:, fast:], func=ACT.Sin, scale=full_turn[:, t : t + 1]
+                out=sine[:, fast:],
+                in_=turns[:, fast:],
+                func=ACT.Sin,
+                scale=full_turn[:, t : t + 1],
+                bias=-math.pi,
             )
             nc.scalar.activation(
                 out=half_sine[:, :fast], in_=frac_of[t][:, :fast], func=ACT.Sin, scale=math.pi
             )
             nc.scalar.activation(
-                out=sine[:, :fast], in_=frac_of[t][:, :fast], func=ACT.Sin, scale=2.0 * math.pi
+                out=sine[:, :fast],
+                in_=frac_of[t][:, :fast],
+                func=ACT.Sin,
+                scale=2.0 * math.pi,
+                bias=-math.pi,
             )
             versine = trig.tile([P, PAIRS], F32)
             nc.scalar.activation(
@@ -283,16 +295,16 @@ def tile_ropeattention_pa_t_kernel(tc, x, w_words, w_scales, out):
                 op0=ALU.subtract,
                 op1=ALU.mult,
             )
+            nc.vector.tensor_tensor(
+                out=crossed[:, 0, pairs], in0=y_pairs[:, :, 1], in1=sine, op=ALU.mult
+            )
             nc.vector.scalar_tensor_tensor(
-                out=crossed[:, 0, pairs],
-                in0=y_pairs[:, :, 1],
+                out=crossed[:, 1, pairs],
+                in0=y_pairs[:, :, 0],
                 scalar=-1.0,
                 in1=sine,
                 op0=ALU.mult,
                 op1=ALU.mult,
-            )
-            nc.vector.tensor_tensor(
-                out=crossed[:, 1, pairs], in0=y_pairs[:, :, 0], in1=sine, op=ALU.mult
             )
             if tensor_subtracts(t, h):
                 return

@@ -360,10 +360,10 @@ def tile_ropeattention_pa_t_kernel(tc, x, w_words, w_scales, out):
         for t in range(FIRST_STEP, TILES):
             if in_range(t - 1) and tensor_subtracts(t - 1, 0):
                 subtract_on_tensor(t - 1, 0)
-            if in_range(t + TRIG_AHEAD):
-                sine_and_versine(t + TRIG_AHEAD)
             if in_range(t + WHOLE_AHEAD):
                 whole_turns(t + WHOLE_AHEAD)
+            if in_range(t + TRIG_AHEAD):
+                sine_and_versine(t + TRIG_AHEAD)
             for flipped_tile in flips_in.get(t, []):
                 flip(flipped_tile)
             if in_range(t - 1) and tensor_subtracts(t - 1, 0):

@@ -38,7 +38,7 @@ DIGIT = 8
 
 def fast_pairs(t):
     last_token = GROUP * P * (t // GROUP) + GROUP * (P - 1) + t % GROUP
-    return min(i for i in range(PAIRS) if last_token * BASE ** (-i / PAIRS) < 2.0 * math.pi)
+    return min(i for i in range(PAIRS) if last_token * BASE ** (-i / PAIRS) < 1.5 * math.pi)
 
 
 WHOLE_AHEAD = 2
@@ -138,8 +138,6 @@ def tile_ropeattention_pa_t_kernel(tc, x, w_words, w_scales, out):
         )
         position = const.tile([P, TILES], F32)
         nc.vector.tensor_copy(out=position[:], in_=position_int[:])
-        half_turn = const.tile([P, TILES], F32)
-        nc.vector.tensor_scalar_mul(out=half_turn[:], in0=position[:], scalar1=math.pi)
         full_turn = const.tile([P, TILES], F32)
         nc.vector.tensor_scalar_mul(out=full_turn[:], in0=position[:], scalar1=2.0 * math.pi)
         turns_columns = const.tile([P, PAIRS // P, P], F32)
@@ -228,10 +226,14 @@ def tile_ropeattention_pa_t_kernel(tc, x, w_words, w_scales, out):
 
         def sine_and_versine(t):
             fast = fast_pairs(t)
-            half_sine = trig.tile([P, PAIRS], F32)
             sine = trig.tile([P, PAIRS], F32)
+            versine = trig.tile([P, PAIRS], F32)
             nc.scalar.activation(
-                out=half_sine[:, fast:], in_=turns[:, fast:], func=ACT.Sin, scale=half_turn[:, t : t + 1]
+                out=versine[:, fast:],
+                in_=turns[:, fast:],
+                func=ACT.Sin,
+                scale=full_turn[:, t : t + 1],
+                bias=-0.5 * math.pi,
             )
             nc.scalar.activation(
                 out=sine[:, fast:],
@@ -240,8 +242,9 @@ def tile_ropeattention_pa_t_kernel(tc, x, w_words, w_scales, out):
                 scale=full_turn[:, t : t + 1],
                 bias=-math.pi,
             )
+            folded = trig.tile([P, PAIRS], F32)
             nc.scalar.activation(
-                out=half_sine[:, :fast], in_=frac_of[t][:, :fast], func=ACT.Sin, scale=math.pi
+                out=folded[:, :fast], in_=frac_of[t][:, :fast], func=ACT.Abs, bias=-0.5
             )
             nc.scalar.activation(
                 out=sine[:, :fast],
@@ -250,9 +253,12 @@ def tile_ropeattention_pa_t_kernel(tc, x, w_words, w_scales, out):
                 scale=2.0 * math.pi,
                 bias=-math.pi,
             )
-            versine = trig.tile([P, PAIRS], F32)
             nc.scalar.activation(
-                out=versine[:], in_=half_sine[:], func=ACT.Square, scale=math.sqrt(2.0)
+                out=versine[:, :fast],
+                in_=folded[:, :fast],
+                func=ACT.Sin,
+                scale=-2.0 * math.pi,
+                bias=0.5 * math.pi,
             )
             sine_of[t] = sine
             versine_of[t] = versine
@@ -287,13 +293,11 @@ def tile_ropeattention_pa_t_kernel(tc, x, w_words, w_scales, out):
             pairs = slice(BANK_PAIRS * h, BANK_PAIRS * (h + 1))
             y_pairs = y_of[(t, h)][:].rearrange("p (i e) -> p i e", e=2)
             sine = sine_of[t][:, pairs]
-            nc.vector.scalar_tensor_tensor(
+            nc.vector.tensor_tensor(
                 out=result[:, pairs, :],
                 in0=versine_of[t][:, pairs].unsqueeze(2).to_broadcast([P, BANK_PAIRS, 2]),
-                scalar=1.0,
                 in1=y_pairs,
-                op0=ALU.subtract,
-                op1=ALU.mult,
+                op=ALU.mult,
             )
             nc.vector.tensor_tensor(
                 out=crossed[:, 0, pairs], in0=y_pairs[:, :, 1], in1=sine, op=ALU.mult

@@ -37,34 +37,41 @@ DIGIT = 8
 
 
 def fast_pairs(t):
+    return pairs_beyond(t, 1.0)
+
+
+def pairs_beyond(t, turns_bound):
     last_token = GROUP * P * (t // GROUP) + GROUP * (P - 1) + t % GROUP
-    return min(i for i in range(PAIRS) if last_token * BASE ** (-i / PAIRS) < 1.5 * math.pi)
+    return min(
+        i for i in range(PAIRS) if last_token * BASE ** (-i / PAIRS) < turns_bound * 2.0 * math.pi
+    )
 
 
-WHOLE_AHEAD = 2
-TRIG_AHEAD = 1
+FRAC_AHEAD = 7
+TRIG_AHEAD = 2
 PROJECT_AHEAD = 1
 FIRST_STEP = -2
-EARLY_TILES = 2
+HEAD_TILES = 5
+FAST_MOST = fast_pairs(TILES - 1)
+FOLDS_MOST = pairs_beyond(TILES - 1, 0.75)
 
 FLOPS = 2 * S * D * D
 
 
-def build_turns_per_token(nc, turns):
-    digits = turns.rearrange("p (a b c) -> p a b c", a=DIGIT, b=DIGIT)
+def build_turns_per_token(nc, turns, one):
     step = BASE ** (-1.0 / PAIRS)
-    nc.vector.memset(turns, 1.0)
-    for a in range(DIGIT):
-        part = digits[:, a, :, :]
+    nc.vector.memset(one, 1.0)
+    for c in range(DIGIT):
         nc.vector.tensor_scalar_mul(
-            out=part, in0=part, scalar1=step ** (DIGIT * DIGIT * a) / (2.0 * math.pi)
+            out=turns[:, c : c + 1], in0=one, scalar1=step**c / (2.0 * math.pi)
         )
-    for b in range(1, DIGIT):
-        part = digits[:, :, b, :]
-        nc.vector.tensor_scalar_mul(out=part, in0=part, scalar1=step ** (DIGIT * b))
-    for c in range(1, DIGIT):
-        part = digits[:, :, :, c]
-        nc.vector.tensor_scalar_mul(out=part, in0=part, scalar1=step**c)
+    for width in (DIGIT, DIGIT * DIGIT):
+        for d in range(1, DIGIT):
+            nc.vector.tensor_scalar_mul(
+                out=turns[:, width * d : width * (d + 1)],
+                in0=turns[:, :width],
+                scalar1=step ** (width * d),
+            )
 
 
 def flips_by_step():
@@ -86,7 +93,10 @@ def tile_ropeattention_pa_t_kernel(tc, x, w_words, w_scales, out):
         stack.enter_context(tc.manual_schedule())
         const = stack.enter_context(tc.tile_pool(name="const", bufs=1))
         quant = stack.enter_context(tc.tile_pool(name="quant", bufs=3))
-        trig = stack.enter_context(tc.tile_pool(name="trig", bufs=4))
+        whole_pool = stack.enter_context(tc.tile_pool(name="whole", bufs=3))
+        frac_pool = stack.enter_context(tc.tile_pool(name="frac", bufs=FRAC_AHEAD - TRIG_AHEAD + 2))
+        fold_pool = stack.enter_context(tc.tile_pool(name="fold", bufs=2))
+        trig = stack.enter_context(tc.tile_pool(name="trig", bufs=TRIG_AHEAD + 2))
         rot = stack.enter_context(tc.tile_pool(name="rot", bufs=8))
         psum_c = stack.enter_context(tc.psum_pool(name="psum_c", bufs=1))
         psum_t = stack.enter_context(tc.psum_pool(name="psum_t", bufs=2))
@@ -111,7 +121,7 @@ def tile_ropeattention_pa_t_kernel(tc, x, w_words, w_scales, out):
         load_x(0)
         load_x(1)
         w_planes = const.tile([P, PASSES, D], U8, align_bytes=64)
-        nc.vector.memset(w_planes[:].bitcast(I32), 0)
+        nc.gpsimd.memset(w_planes[:].bitcast(F32), 0.0)
         for q in range(4):
             nc.sync.dma_start(
                 out=w_planes[32 * q : 32 * q + 4, :, :].bitcast(I32),
@@ -124,35 +134,46 @@ def tile_ropeattention_pa_t_kernel(tc, x, w_words, w_scales, out):
             load_x(c)
 
         turns = const.tile([P, PAIRS], F32)
-        build_turns_per_token(nc, turns[:])
-        ident = const.tile([P, P], F32)
-        make_identity(nc, ident[:])
-        minus_ident = const.tile([P, P], F32)
-        nc.vector.tensor_scalar_mul(out=minus_ident[:], in0=ident[:], scalar1=-1.0)
-        position_int = const.tile([P, TILES], I32)
+        one = const.tile([P, 1], F32)
+        build_turns_per_token(nc, turns[:], one[:])
+        position = const.tile([P, TILES], F32)
         nc.gpsimd.iota(
-            out=position_int[:],
+            out=position[:],
             pattern=[[GROUP * P, TILES // GROUP], [1, GROUP]],
             base=0,
             channel_multiplier=GROUP,
+            allow_small_or_imprecise_dtypes=True,
         )
-        position = const.tile([P, TILES], F32)
-        nc.vector.tensor_copy(out=position[:], in_=position_int[:])
         full_turn = const.tile([P, TILES], F32)
-        nc.vector.tensor_scalar_mul(out=full_turn[:], in0=position[:], scalar1=2.0 * math.pi)
-        turns_columns = const.tile([P, PAIRS // P, P], F32)
+        nc.gpsimd.tensor_scalar(
+            out=full_turn[:],
+            in0=position[:],
+            scalar1=2.0 * math.pi,
+            scalar2=0.0,
+            op0=ALU.mult,
+            op1=ALU.add,
+        )
+        ident = const.tile([P, P], F32)
+        make_identity(nc, ident[:])
+        minus_ident = const.tile([P, P], F32)
+        nc.gpsimd.tensor_scalar(
+            out=minus_ident[:], in0=ident[:], scalar1=-1.0, scalar2=0.0, op0=ALU.mult, op1=ALU.add
+        )
+        turns_column = const.tile([P, PAIRS // P], F32)
         turns_psum = psum_c.tile([P, PAIRS], F32)
 
         def turns_to_columns():
             turns_flipped = psum_t.tile([P, PAIRS // P, P], F32, tag="flipped")
             for b in range(PAIRS // P):
                 nc.tensor.transpose(turns_flipped[:, b, :], turns[:, b * P : (b + 1) * P], ident[:])
-            nc.vector.tensor_copy(out=turns_columns[:], in_=turns_flipped[:])
+            nc.vector.tensor_copy(out=turns_column[:], in_=turns_flipped[:, :, 0])
 
         def columns_to_psum():
             for b in range(PAIRS // P):
                 nc.tensor.transpose(
-                    turns_psum[:, b * P : (b + 1) * P], turns_columns[:, b, :], ident[:]
+                    turns_psum[:, b * P : (b + 1) * P],
+                    turns_column[:, b : b + 1].to_broadcast([P, P]),
+                    ident[:],
                 )
 
         chunk_of = {}
@@ -201,22 +222,32 @@ def tile_ropeattention_pa_t_kernel(tc, x, w_words, w_scales, out):
 
         def whole_turns(t):
             fast = fast_pairs(t)
-            whole = trig.tile([P, PAIRS], U32)
-            nc.scalar.activation(
-                out=whole[:, :fast],
-                in_=turns[:, :fast],
-                func=ACT.Copy,
-                scale=position[:, t : t + 1],
-                bias=-0.5,
-            )
+            whole = whole_pool.tile([P, FAST_MOST], U32)
+            if t < FRAC_AHEAD:
+                nc.vector.tensor_scalar(
+                    out=whole[:, :fast].bitcast(I32),
+                    in0=turns[:, :fast],
+                    scalar1=position[:, t : t + 1],
+                    scalar2=-0.5,
+                    op0=ALU.mult,
+                    op1=ALU.add,
+                )
+            else:
+                nc.scalar.activation(
+                    out=whole[:, :fast],
+                    in_=turns[:, :fast],
+                    func=ACT.Copy,
+                    scale=position[:, t : t + 1],
+                    bias=-0.5,
+                )
             whole_of[t] = whole
 
         def fraction(t):
             fast = fast_pairs(t)
-            frac = trig.tile([P, PAIRS], F32)
+            frac = frac_pool.tile([P, FAST_MOST], F32)
             nc.vector.scalar_tensor_tensor(
                 out=frac[:, :fast],
-                in0=(turns if t < EARLY_TILES else turns_psum)[:, :fast],
+                in0=(turns if t < FRAC_AHEAD else turns_psum)[:, :fast],
                 scalar=position[:, t : t + 1],
                 in1=whole_of[t][:, :fast].bitcast(I32),
                 op0=ALU.mult,
@@ -224,13 +255,22 @@ def tile_ropeattention_pa_t_kernel(tc, x, w_words, w_scales, out):
             )
             frac_of[t] = frac
 
+        def early_fractions(tiles):
+            for n in range(len(tiles)):
+                whole_turns(tiles[n])
+                if n > 0:
+                    fraction(tiles[n - 1])
+            fraction(tiles[-1])
+
         def sine_and_versine(t):
             fast = fast_pairs(t)
+            folds = pairs_beyond(t, 0.75)
             sine = trig.tile([P, PAIRS], F32)
             versine = trig.tile([P, PAIRS], F32)
+            folded = fold_pool.tile([P, FOLDS_MOST], F32)
             nc.scalar.activation(
-                out=versine[:, fast:],
-                in_=turns[:, fast:],
+                out=versine[:, folds:],
+                in_=turns[:, folds:],
                 func=ACT.Sin,
                 scale=full_turn[:, t : t + 1],
                 bias=-0.5 * math.pi,
@@ -242,7 +282,13 @@ def tile_ropeattention_pa_t_kernel(tc, x, w_words, w_scales, out):
                 scale=full_turn[:, t : t + 1],
                 bias=-math.pi,
             )
-            folded = trig.tile([P, PAIRS], F32)
+            nc.scalar.activation(
+                out=folded[:, fast:folds],
+                in_=turns[:, fast:folds],
+                func=ACT.Abs,
+                scale=position[:, t : t + 1],
+                bias=-0.5,
+            )
             nc.scalar.activation(
                 out=folded[:, :fast], in_=frac_of[t][:, :fast], func=ACT.Abs, bias=-0.5
             )
@@ -254,8 +300,8 @@ def tile_ropeattention_pa_t_kernel(tc, x, w_words, w_scales, out):
                 bias=-math.pi,
             )
             nc.scalar.activation(
-                out=versine[:, :fast],
-                in_=folded[:, :fast],
+                out=versine[:, :folds],
+                in_=folded[:, :folds],
                 func=ACT.Sin,
                 scale=-2.0 * math.pi,
                 bias=0.5 * math.pi,
@@ -362,10 +408,12 @@ def tile_ropeattention_pa_t_kernel(tc, x, w_words, w_scales, out):
 
         flips_in = flips_by_step()
         for t in range(FIRST_STEP, TILES):
+            if t == FIRST_STEP:
+                early_fractions(list(range(HEAD_TILES)))
             if in_range(t - 1) and tensor_subtracts(t - 1, 0):
                 subtract_on_tensor(t - 1, 0)
-            if in_range(t + WHOLE_AHEAD):
-                whole_turns(t + WHOLE_AHEAD)
+            if in_range(t) and in_range(t + FRAC_AHEAD):
+                whole_turns(t + FRAC_AHEAD)
             if in_range(t + TRIG_AHEAD):
                 sine_and_versine(t + TRIG_AHEAD)
             for flipped_tile in flips_in.get(t, []):
@@ -377,6 +425,7 @@ def tile_ropeattention_pa_t_kernel(tc, x, w_words, w_scales, out):
             if t + PROJECT_AHEAD in CHUNK_FIRST:
                 quantise(chunk_of[t + PROJECT_AHEAD])
             if t == FIRST_STEP + 1:
+                early_fractions(list(range(HEAD_TILES, FRAC_AHEAD)))
                 turns_to_columns()
             if in_range(t + PROJECT_AHEAD):
                 project(t + PROJECT_AHEAD)
@@ -384,5 +433,5 @@ def tile_ropeattention_pa_t_kernel(tc, x, w_words, w_scales, out):
                 columns_to_psum()
             if in_range(t):
                 rotate_and_store(t, 1)
-            if in_range(t + WHOLE_AHEAD):
-                fraction(t + WHOLE_AHEAD)
+            if in_range(t) and in_range(t + FRAC_AHEAD):
+                fraction(t + FRAC_AHEAD)

@@ -52,6 +52,8 @@ TRIG_AHEAD = 2
 PROJECT_AHEAD = 1
 FIRST_STEP = -2
 HEAD_TILES = 5
+IDLE_FIRST = 3
+IDLE_SECOND = 2
 FAST_MOST = fast_pairs(TILES - 1)
 FOLDS_MOST = pairs_beyond(TILES - 1, 0.75)
 
@@ -121,7 +123,7 @@ def tile_ropeattention_pa_t_kernel(tc, x, w_words, w_scales, out):
         load_x(0)
         load_x(1)
         w_planes = const.tile([P, PASSES, D], U8, align_bytes=64)
-        nc.gpsimd.memset(w_planes[:].bitcast(F32), 0.0)
+        nc.vector.memset(w_planes[:].bitcast(I32), 0)
         for q in range(4):
             nc.sync.dma_start(
                 out=w_planes[32 * q : 32 * q + 4, :, :].bitcast(I32),
@@ -133,6 +135,8 @@ def tile_ropeattention_pa_t_kernel(tc, x, w_words, w_scales, out):
         for c in range(2, CHUNKS):
             load_x(c)
 
+        ident = const.tile([P, P], F32)
+        make_identity(nc, ident[:])
         turns = const.tile([P, PAIRS], F32)
         one = const.tile([P, 1], F32)
         build_turns_per_token(nc, turns[:], one[:])
@@ -153,12 +157,16 @@ def tile_ropeattention_pa_t_kernel(tc, x, w_words, w_scales, out):
             op0=ALU.mult,
             op1=ALU.add,
         )
-        ident = const.tile([P, P], F32)
-        make_identity(nc, ident[:])
         minus_ident = const.tile([P, P], F32)
         nc.gpsimd.tensor_scalar(
             out=minus_ident[:], in0=ident[:], scalar1=-1.0, scalar2=0.0, op0=ALU.mult, op1=ALU.add
         )
+        def multiply_idly(count):
+            idle_out = psum_s.tile([P, P], F32, tag="difference")
+            for n in range(count):
+                nc.tensor.matmul(out=idle_out[:], lhsT=ident[:], rhs=ident[:], start=True, stop=True)
+
+        multiply_idly(IDLE_FIRST)
         turns_column = const.tile([P, PAIRS // P], F32)
         turns_psum = psum_c.tile([P, PAIRS], F32)
 
@@ -375,6 +383,8 @@ def tile_ropeattention_pa_t_kernel(tc, x, w_words, w_scales, out):
             )
 
         def tensor_subtracts(t, h):
+            if h == 0 and t == TILES - CHUNK:
+                return True
             return h == 0 and t % CHUNK == CHUNK - 2
 
         difference_of = {}
@@ -410,6 +420,9 @@ def tile_ropeattention_pa_t_kernel(tc, x, w_words, w_scales, out):
         for t in range(FIRST_STEP, TILES):
             if t == FIRST_STEP:
                 early_fractions(list(range(HEAD_TILES)))
+            late = t >= TILES - CHUNK
+            if late and in_range(t + PROJECT_AHEAD):
+                project(t + PROJECT_AHEAD)
             if in_range(t - 1) and tensor_subtracts(t - 1, 0):
                 subtract_on_tensor(t - 1, 0)
             if in_range(t) and in_range(t + FRAC_AHEAD):
@@ -427,7 +440,8 @@ def tile_ropeattention_pa_t_kernel(tc, x, w_words, w_scales, out):
             if t == FIRST_STEP + 1:
                 early_fractions(list(range(HEAD_TILES, FRAC_AHEAD)))
                 turns_to_columns()
-            if in_range(t + PROJECT_AHEAD):
+                multiply_idly(IDLE_SECOND)
+            if in_range(t + PROJECT_AHEAD) and not late:
                 project(t + PROJECT_AHEAD)
             if t == FIRST_STEP + 1:
                 columns_to_psum()

@@ -36,15 +36,44 @@ BASE = 10000.0
 DIGIT = 8
 
 
+RUNS_MOST = 5
+MARGIN = 1.0e-3
+
+
+def fits(t, i, shift, k):
+    first_token = GROUP * P * (t // GROUP) + t % GROUP
+    last_token = first_token + GROUP * (P - 1)
+    per_token = BASE ** (-i / PAIRS)
+    lowest = first_token * per_token - shift - k * math.pi
+    highest = last_token * per_token - shift - k * math.pi
+    return lowest >= -math.pi + (MARGIN if k > 0 else 0.0) and highest <= math.pi - MARGIN
+
+
+def direct_runs(t, shift):
+    runs = []
+    k = 0
+    end = PAIRS
+    for i in range(PAIRS - 1, -1, -1):
+        if fits(t, i, shift, k):
+            continue
+        runs.append((i + 1, end, k))
+        end = i + 1
+        if len(runs) == RUNS_MOST or not fits(t, i, shift, k + 1):
+            return runs
+        k += 1
+    runs.append((0, end, k))
+    return runs
+
+
 def fast_pairs(t):
-    return pairs_beyond(t, 1.0)
+    sine_from = direct_runs(t, math.pi)[-1][0]
+    if len(direct_runs(t, math.pi)) == 1:
+        return sine_from
+    return max(sine_from, direct_runs(t, 0.5 * math.pi)[-1][0])
 
 
-def pairs_beyond(t, turns_bound):
-    last_token = GROUP * P * (t // GROUP) + GROUP * (P - 1) + t % GROUP
-    return min(
-        i for i in range(PAIRS) if last_token * BASE ** (-i / PAIRS) < turns_bound * 2.0 * math.pi
-    )
+def fold_pairs(t):
+    return max(fast_pairs(t), direct_runs(t, 0.5 * math.pi)[-1][0])
 
 
 FRAC_AHEAD = 7
@@ -54,8 +83,8 @@ FIRST_STEP = -2
 HEAD_TILES = 5
 IDLE_FIRST = 3
 IDLE_SECOND = 2
-FAST_MOST = fast_pairs(TILES - 1)
-FOLDS_MOST = pairs_beyond(TILES - 1, 0.75)
+FAST_MOST = max(fast_pairs(t) for t in range(TILES))
+FOLDS_MOST = max(fold_pairs(t) for t in range(TILES))
 
 FLOPS = 2 * S * D * D
 
@@ -153,6 +182,15 @@ def tile_ropeattention_pa_t_kernel(tc, x, w_words, w_scales, out):
             out=full_turn[:],
             in0=position[:],
             scalar1=2.0 * math.pi,
+            scalar2=0.0,
+            op0=ALU.mult,
+            op1=ALU.add,
+        )
+        minus_full_turn = const.tile([P, TILES], F32)
+        nc.gpsimd.tensor_scalar(
+            out=minus_full_turn[:],
+            in0=position[:],
+            scalar1=-2.0 * math.pi,
             scalar2=0.0,
             op0=ALU.mult,
             op1=ALU.add,
@@ -272,31 +310,31 @@ def tile_ropeattention_pa_t_kernel(tc, x, w_words, w_scales, out):
 
         def sine_and_versine(t):
             fast = fast_pairs(t)
-            folds = pairs_beyond(t, 0.75)
+            folds = fold_pairs(t)
             sine = trig.tile([P, PAIRS], F32)
             versine = trig.tile([P, PAIRS], F32)
             folded = fold_pool.tile([P, FOLDS_MOST], F32)
-            nc.scalar.activation(
-                out=versine[:, folds:],
-                in_=turns[:, folds:],
-                func=ACT.Sin,
-                scale=full_turn[:, t : t + 1],
-                bias=-0.5 * math.pi,
-            )
-            nc.scalar.activation(
-                out=sine[:, fast:],
-                in_=turns[:, fast:],
-                func=ACT.Sin,
-                scale=full_turn[:, t : t + 1],
-                bias=-math.pi,
-            )
-            nc.scalar.activation(
-                out=folded[:, fast:folds],
-                in_=turns[:, fast:folds],
-                func=ACT.Abs,
-                scale=position[:, t : t + 1],
-                bias=-0.5,
-            )
+            for table, shift, first_pair in ((versine, 0.5 * math.pi, folds), (sine, math.pi, fast)):
+                for run_first, run_end, k in direct_runs(t, shift):
+                    run = slice(max(run_first, first_pair), run_end)
+                    if run.start >= run.stop:
+                        continue
+                    odd = k % 2 == 1
+                    nc.scalar.activation(
+                        out=table[:, run],
+                        in_=turns[:, run],
+                        func=ACT.Sin,
+                        scale=(minus_full_turn if odd else full_turn)[:, t : t + 1],
+                        bias=(shift + k * math.pi) * (1.0 if odd else -1.0),
+                    )
+            if folds > fast:
+                nc.scalar.activation(
+                    out=folded[:, fast:folds],
+                    in_=turns[:, fast:folds],
+                    func=ACT.Abs,
+                    scale=position[:, t : t + 1],
+                    bias=-0.5,
+                )
             nc.scalar.activation(
                 out=folded[:, :fast], in_=frac_of[t][:, :fast], func=ACT.Abs, bias=-0.5
             )

@@ -25,7 +25,6 @@ BANKS_OUT = D // BANK
 PAIRS = D // 2
 BANK_PAIRS = BANK // 2
 TILES = S // P
-GROUP = 4
 CHUNK = 4
 CHUNK_TILES = (1, 1, 2) + (CHUNK,) * 7
 assert sum(CHUNK_TILES) == TILES
@@ -36,13 +35,13 @@ BASE = 10000.0
 DIGIT = 8
 
 
-RUNS_MOST = 5
+RUNS_MOST = 8
 MARGIN = 1.0e-3
 
 
 def fits(t, i, shift, k):
-    first_token = GROUP * P * (t // GROUP) + t % GROUP
-    last_token = first_token + GROUP * (P - 1)
+    first_token = P * t
+    last_token = first_token + P - 1
     per_token = BASE ** (-i / PAIRS)
     lowest = first_token * per_token - shift - k * math.pi
     highest = last_token * per_token - shift - k * math.pi
@@ -117,8 +116,8 @@ def flips_by_step():
 
 def tile_ropeattention_pa_t_kernel(tc, x, w_words, w_scales, out):
     nc = tc.nc
-    x_groups = x.rearrange("(c p j) k -> p c j k", p=P, j=GROUP)
-    out_groups = out.rearrange("(c p j) n -> p c j n", p=P, j=GROUP)
+    x_tiles = x.rearrange("(t p) k -> p t k", p=P)
+    out_tiles = out.rearrange("(t p) n -> p t n", p=P)
 
     with ExitStack() as stack:
         stack.enter_context(tc.manual_schedule())
@@ -145,8 +144,7 @@ def tile_ropeattention_pa_t_kernel(tc, x, w_words, w_scales, out):
             first = CHUNK_FIRST[c]
             count = CHUNK_TILES[c]
             nc.sync.dma_start(
-                out=x_all[:, first : first + count, :],
-                in_=x_groups[:, first // GROUP, first % GROUP : first % GROUP + count, :],
+                out=x_all[:, first : first + count, :], in_=x_tiles[:, first : first + count, :]
             )
 
         load_x(0)
@@ -172,9 +170,9 @@ def tile_ropeattention_pa_t_kernel(tc, x, w_words, w_scales, out):
         position = const.tile([P, TILES], F32)
         nc.gpsimd.iota(
             out=position[:],
-            pattern=[[GROUP * P, TILES // GROUP], [1, GROUP]],
+            pattern=[[P, TILES]],
             base=0,
-            channel_multiplier=GROUP,
+            channel_multiplier=1,
             allow_small_or_imprecise_dtypes=True,
         )
         full_turn = const.tile([P, TILES], F32)
@@ -416,7 +414,7 @@ def tile_ropeattention_pa_t_kernel(tc, x, w_words, w_scales, out):
         def store(t, h):
             pairs = slice(BANK_PAIRS * h, BANK_PAIRS * (h + 1))
             nc.sync.dma_start(
-                out=out_groups[:, t // GROUP, t % GROUP, BANK * h : BANK * (h + 1)],
+                out=out_tiles[:, t, BANK * h : BANK * (h + 1)],
                 in_=result_of[t][:, pairs, :].rearrange("p i e -> p (i e)"),
             )
 

import math
from contextlib import ExitStack

import concourse.mybir as mybir
from concourse.masks import make_identity

F32 = mybir.dt.float32
BF16 = mybir.dt.bfloat16
I32 = mybir.dt.int32
U32 = mybir.dt.uint32
U8 = mybir.dt.uint8
FP8X4 = mybir.dt.float8_e4m3fn_x4
FP4X4 = mybir.dt.float4_e2m1fn_x4
ALU = mybir.AluOpType
ACT = mybir.ActivationFunctionType

S = 4096
D = 1024
P = 128
PACK = 4
K_PASS = P * PACK
PASSES = D // K_PASS
BANK = 512
BANKS_OUT = D // BANK
PAIRS = D // 2
BANK_PAIRS = BANK // 2
TILES = S // P
CHUNK = 4
CHUNK_TILES = (1, 1, 2) + (CHUNK,) * 7
assert sum(CHUNK_TILES) == TILES
CHUNKS = len(CHUNK_TILES)
CHUNK_FIRST = tuple(sum(CHUNK_TILES[:c]) for c in range(CHUNKS))
TILE_WORDS = PASSES * P
BASE = 10000.0
DIGIT = 8


RUNS_MOST = 8
MARGIN = 1.0e-3


def fits(t, i, shift, k):
    first_token = P * t
    last_token = first_token + P - 1
    per_token = BASE ** (-i / PAIRS)
    lowest = first_token * per_token - shift - k * math.pi
    highest = last_token * per_token - shift - k * math.pi
    return lowest >= -math.pi + (MARGIN if k > 0 else 0.0) and highest <= math.pi - MARGIN


def direct_runs(t, shift):
    runs = []
    k = 0
    end = PAIRS
    for i in range(PAIRS - 1, -1, -1):
        if fits(t, i, shift, k):
            continue
        runs.append((i + 1, end, k))
        end = i + 1
        if len(runs) == RUNS_MOST or not fits(t, i, shift, k + 1):
            return runs
        k += 1
    runs.append((0, end, k))
    return runs


def fast_pairs(t):
    sine_from = direct_runs(t, math.pi)[-1][0]
    if len(direct_runs(t, math.pi)) == 1:
        return sine_from
    return max(sine_from, direct_runs(t, 0.5 * math.pi)[-1][0])


def fold_pairs(t):
    return max(fast_pairs(t), direct_runs(t, 0.5 * math.pi)[-1][0])


FRAC_AHEAD = 7
TRIG_AHEAD = 2
PROJECT_AHEAD = 1
FIRST_STEP = -2
HEAD_TILES = 5
IDLE_FIRST = 3
IDLE_SECOND = 2
FAST_MOST = max(fast_pairs(t) for t in range(TILES))
FOLDS_MOST = max(fold_pairs(t) for t in range(TILES))

FLOPS = 2 * S * D * D


def build_turns_per_token(nc, turns, one):
    step = BASE ** (-1.0 / PAIRS)
    nc.vector.memset(one, 1.0)
    for c in range(DIGIT):
        nc.vector.tensor_scalar_mul(
            out=turns[:, c : c + 1], in0=one, scalar1=step**c / (2.0 * math.pi)
        )
    for width in (DIGIT, DIGIT * DIGIT):
        for d in range(1, DIGIT):
            nc.vector.tensor_scalar_mul(
                out=turns[:, width * d : width * (d + 1)],
                in0=turns[:, :width],
                scalar1=step ** (width * d),
            )


def flips_by_step():
    plan = {FIRST_STEP: list(range(CHUNK_TILES[0]))}
    for c in range(1, CHUNKS):
        steps = CHUNK_TILES[c - 1]
        a_step = -(-CHUNK_TILES[c] // steps)
        for j in range(CHUNK_TILES[c]):
            plan.setdefault(CHUNK_FIRST[c] - 1 - steps + j // a_step, []).append(CHUNK_FIRST[c] + j)
    return plan


def tile_ropeattention_pa_t_kernel(tc, x, w_words, w_scales, out):
    nc = tc.nc
    x_tiles = x.rearrange("(t p) k -> p t k", p=P)
    out_tiles = out.rearrange("(t p) n -> p t n", p=P)

    with ExitStack() as stack:
        stack.enter_context(tc.manual_schedule())
        const = stack.enter_context(tc.tile_pool(name="const", bufs=1))
        quant = stack.enter_context(tc.tile_pool(name="quant", bufs=3))
        whole_pool = stack.enter_context(tc.tile_pool(name="whole", bufs=3))
        frac_pool = stack.enter_context(tc.tile_pool(name="frac", bufs=FRAC_AHEAD - TRIG_AHEAD + 2))
        fold_pool = stack.enter_context(tc.tile_pool(name="fold", bufs=2))
        trig = stack.enter_context(tc.tile_pool(name="trig", bufs=TRIG_AHEAD + 2))
        rot = stack.enter_context(tc.tile_pool(name="rot", bufs=8))
        psum_c = stack.enter_context(tc.psum_pool(name="psum_c", bufs=1))
        psum_t = stack.enter_context(tc.psum_pool(name="psum_t", bufs=2))
        psum_y = stack.enter_context(tc.psum_pool(name="psum_y", bufs=4))
        psum_s = stack.enter_context(tc.psum_pool(name="psum_s", bufs=1))

        zero = const.tile([P, 1], F32)
        nc.gpsimd.memset(zero[:], 0.0)
        unused = const.tile([P, 1], F32)
        nc.scalar.activation(out=unused[:], in_=zero[:], func=ACT.Sin)

        x_all = const.tile([P, TILES, D], BF16)

        def load_x(c):
            first = CHUNK_FIRST[c]
            count = CHUNK_TILES[c]
            nc.sync.dma_start(
                out=x_all[:, first : first + count, :], in_=x_tiles[:, first : first + count, :]
            )

        load_x(0)
        load_x(1)
        w_planes = const.tile([P, PASSES, D], U8, align_bytes=64)
        nc.vector.memset(w_planes[:].bitcast(I32), 0)
        for q in range(4):
            nc.sync.dma_start(
                out=w_planes[32 * q : 32 * q + 4, :, :].bitcast(I32),
                in_=w_scales[:, 4 * q : 4 * q + 4, :].rearrange("g r n -> r g n").bitcast(I32),
            )
        w_codes = const.tile([P, PASSES, 2 * D], U8, align_bytes=64)
        for g in range(PASSES):
            nc.sync.dma_start(out=w_codes[:, g, :].bitcast(I32), in_=w_words[g].bitcast(I32))
        for c in range(2, CHUNKS):
            load_x(c)

        ident = const.tile([P, P], F32)
        make_identity(nc, ident[:])
        turns = const.tile([P, PAIRS], F32)
        one = const.tile([P, 1], F32)
        build_turns_per_token(nc, turns[:], one[:])
        position = const.tile([P, TILES], F32)
        nc.gpsimd.iota(
            out=position[:],
            pattern=[[P, TILES]],
            base=0,
            channel_multiplier=1,
            allow_small_or_imprecise_dtypes=True,
        )
        full_turn = const.tile([P, TILES], F32)
        nc.gpsimd.tensor_scalar(
            out=full_turn[:],
            in0=position[:],
            scalar1=2.0 * math.pi,
            scalar2=0.0,
            op0=ALU.mult,
            op1=ALU.add,
        )
        minus_full_turn = const.tile([P, TILES], F32)
        nc.gpsimd.tensor_scalar(
            out=minus_full_turn[:],
            in0=position[:],
            scalar1=-2.0 * math.pi,
            scalar2=0.0,
            op0=ALU.mult,
            op1=ALU.add,
        )
        minus_ident = const.tile([P, P], F32)
        nc.gpsimd.tensor_scalar(
            out=minus_ident[:], in0=ident[:], scalar1=-1.0, scalar2=0.0, op0=ALU.mult, op1=ALU.add
        )
        def multiply_idly(count):
            idle_out = psum_s.tile([P, P], F32, tag="difference")
            for n in range(count):
                nc.tensor.matmul(out=idle_out[:], lhsT=ident[:], rhs=ident[:], start=True, stop=True)

        multiply_idly(IDLE_FIRST)
        turns_column = const.tile([P, PAIRS // P], F32)
        turns_psum = psum_c.tile([P, PAIRS], F32)

        def turns_to_columns():
            turns_flipped = psum_t.tile([P, PAIRS // P, P], F32, tag="flipped")
            for b in range(PAIRS // P):
                nc.tensor.transpose(turns_flipped[:, b, :], turns[:, b * P : (b + 1) * P], ident[:])
            nc.vector.tensor_copy(out=turns_column[:], in_=turns_flipped[:, :, 0])

        def columns_to_psum():
            for b in range(PAIRS // P):
                nc.tensor.transpose(
                    turns_psum[:, b * P : (b + 1) * P],
                    turns_column[:, b : b + 1].to_broadcast([P, P]),
                    ident[:],
                )

        chunk_of = {}
        for c in range(CHUNKS):
            for j in range(CHUNK_TILES[c]):
                chunk_of[CHUNK_FIRST[c] + j] = c
        grouped_of = {}
        x_codes_of = {}
        x_planes_of = {}
        whole_of = {}
        frac_of = {}
        sine_of = {}
        versine_of = {}
        y_of = {}
        result_of = {}
        crossed_of = {}

        def flip(t):
            c = chunk_of[t]
            x_words = x_all[:, t, :].bitcast(F32)
            flipped = psum_t.tile([P, PASSES, 2, P], F32)
            for g in range(PASSES):
                for u in range(2):
                    nc.tensor.transpose(
                        flipped[:, g, u, :], x_words[:, 256 * g + u : 256 * (g + 1) : 2], ident[:]
                    )
            if t == CHUNK_FIRST[c]:
                grouped = quant.tile([P, CHUNK, PASSES, P, PACK], BF16, align_bytes=64)
                grouped_of[c] = grouped
            nc.scalar.copy(
                out=grouped_of[c][:, t - CHUNK_FIRST[c]].bitcast(F32),
                in_=flipped[:].rearrange("p g u r -> p g r u"),
            )

        def quantise(c):
            words = CHUNK_TILES[c] * TILE_WORDS
            x_codes = quant.tile([P, CHUNK * TILE_WORDS], U32, align_bytes=64)
            x_planes = quant.tile([P, CHUNK * TILE_WORDS], U8, align_bytes=64)
            nc.vector.quantize_mx(
                out=x_codes[:, :words].bitcast(FP8X4),
                scales=x_planes[:, :words],
                in_=grouped_of[c][:, : CHUNK_TILES[c]].rearrange("p t g r j -> p (t g r j)"),
            )
            x_codes_of[c] = x_codes
            x_planes_of[c] = x_planes

        def whole_turns(t):
            fast = fast_pairs(t)
            whole = whole_pool.tile([P, FAST_MOST], U32)
            if t < FRAC_AHEAD:
                nc.vector.tensor_scalar(
                    out=whole[:, :fast].bitcast(I32),
                    in0=turns[:, :fast],
                    scalar1=position[:, t : t + 1],
                    scalar2=-0.5,
                    op0=ALU.mult,
                    op1=ALU.add,
                )
            else:
                nc.scalar.activation(
                    out=whole[:, :fast],
                    in_=turns[:, :fast],
                    func=ACT.Copy,
                    scale=position[:, t : t + 1],
                    bias=-0.5,
                )
            whole_of[t] = whole

        def fraction(t):
            fast = fast_pairs(t)
            frac = frac_pool.tile([P, FAST_MOST], F32)
            nc.vector.scalar_tensor_tensor(
                out=frac[:, :fast],
                in0=(turns if t < FRAC_AHEAD else turns_psum)[:, :fast],
                scalar=position[:, t : t + 1],
                in1=whole_of[t][:, :fast].bitcast(I32),
                op0=ALU.mult,
                op1=ALU.subtract,
            )
            frac_of[t] = frac

        def early_fractions(tiles):
            for n in range(len(tiles)):
                whole_turns(tiles[n])
                if n > 0:
                    fraction(tiles[n - 1])
            fraction(tiles[-1])

        def sine_and_versine(t):
            fast = fast_pairs(t)
            folds = fold_pairs(t)
            sine = trig.tile([P, PAIRS], F32)
            versine = trig.tile([P, PAIRS], F32)
            folded = fold_pool.tile([P, FOLDS_MOST], F32)
            for table, shift, first_pair in ((versine, 0.5 * math.pi, folds), (sine, math.pi, fast)):
                for run_first, run_end, k in direct_runs(t, shift):
                    run = slice(max(run_first, first_pair), run_end)
                    if run.start >= run.stop:
                        continue
                    odd = k % 2 == 1
                    nc.scalar.activation(
                        out=table[:, run],
                        in_=turns[:, run],
                        func=ACT.Sin,
                        scale=(minus_full_turn if odd else full_turn)[:, t : t + 1],
                        bias=(shift + k * math.pi) * (1.0 if odd else -1.0),
                    )
            if folds > fast:
                nc.scalar.activation(
                    out=folded[:, fast:folds],
                    in_=turns[:, fast:folds],
                    func=ACT.Abs,
                    scale=position[:, t : t + 1],
                    bias=-0.5,
                )
            nc.scalar.activation(
                out=folded[:, :fast], in_=frac_of[t][:, :fast], func=ACT.Abs, bias=-0.5
            )
            nc.scalar.activation(
                out=sine[:, :fast],
                in_=frac_of[t][:, :fast],
                func=ACT.Sin,
                scale=2.0 * math.pi,
                bias=-math.pi,
            )
            nc.scalar.activation(
                out=versine[:, :folds],
                in_=folded[:, :folds],
                func=ACT.Sin,
                scale=-2.0 * math.pi,
                bias=0.5 * math.pi,
            )
            sine_of[t] = sine
            versine_of[t] = versine

        def project(t):
            c = chunk_of[t]
            first_word = (t - CHUNK_FIRST[c]) * TILE_WORDS
            x_codes = x_codes_of[c][:, first_word : first_word + TILE_WORDS]
            x_planes = x_planes_of[c][:, first_word : first_word + TILE_WORDS]
            for h in range(BANKS_OUT):
                y = psum_y.tile([P, BANK], F32)
                for g in range(PASSES):
                    nc.tensor.matmul_mx(
                        out=y[:],
                        lhsT=x_codes[:, g * P : (g + 1) * P].bitcast(FP8X4),
                        lhsT_scale=x_planes[:, g * P : (g + 1) * P],
                        rhs=w_codes[:, g, 2 * BANK * h : 2 * BANK * (h + 1)].bitcast(FP4X4),
                        rhs_scale=w_planes[:, g, BANK * h : BANK * (h + 1)],
                        start=(g == 0),
                        stop=(g == PASSES - 1),
                    )
                y_of[(t, h)] = y

        def rotate_and_store(t, h):
            if h == 0:
                result = rot.tile([P, PAIRS, 2], F32)
                crossed = rot.tile([P, 2, PAIRS], F32)
                result_of[t] = result
                crossed_of[t] = crossed
            result = result_of[t]
            crossed = crossed_of[t]
            pairs = slice(BANK_PAIRS * h, BANK_PAIRS * (h + 1))
            y_pairs = y_of[(t, h)][:].rearrange("p (i e) -> p i e", e=2)
            sine = sine_of[t][:, pairs]
            nc.vector.tensor_tensor(
                out=result[:, pairs, :],
                in0=versine_of[t][:, pairs].unsqueeze(2).to_broadcast([P, BANK_PAIRS, 2]),
                in1=y_pairs,
                op=ALU.mult,
            )
            nc.vector.tensor_tensor(
                out=crossed[:, 0, pairs], in0=y_pairs[:, :, 1], in1=sine, op=ALU.mult
            )
            nc.vector.scalar_tensor_tensor(
                out=crossed[:, 1, pairs],
                in0=y_pairs[:, :, 0],
                scalar=-1.0,
                in1=sine,
                op0=ALU.mult,
                op1=ALU.mult,
            )
            if tensor_subtracts(t, h):
                return
            subtractor = nc.vector if (t, h) == (TILES - 1, BANKS_OUT - 1) else nc.gpsimd
            subtractor.tensor_tensor(
                out=result[:, pairs, :],
                in0=crossed[:, :, pairs].rearrange("p e i -> p i e"),
                in1=result[:, pairs, :],
                op=ALU.subtract,
            )
            store(t, h)

        def store(t, h):
            pairs = slice(BANK_PAIRS * h, BANK_PAIRS * (h + 1))
            nc.sync.dma_start(
                out=out_tiles[:, t, BANK * h : BANK * (h + 1)],
                in_=result_of[t][:, pairs, :].rearrange("p i e -> p (i e)"),
            )

        def tensor_subtracts(t, h):
            if h == 0 and t == TILES - CHUNK:
                return True
            return h == 0 and t % CHUNK == CHUNK - 2

        difference_of = {}

        def subtract_on_tensor(t, h):
            pairs = slice(BANK_PAIRS * h, BANK_PAIRS * (h + 1))
            difference = psum_s.tile([P, BANK_PAIRS, 2], F32)
            nc.tensor.matmul(
                out=difference[:],
                lhsT=ident[:],
                rhs=crossed_of[t][:, :, pairs].rearrange("p e i -> p i e"),
                start=True,
                stop=False,
            )
            nc.tensor.matmul(
                out=difference[:],
                lhsT=minus_ident[:],
                rhs=result_of[t][:, pairs, :],
                start=False,
                stop=True,
            )
            difference_of[(t, h)] = difference

        def copy_difference_and_store(t, h):
            pairs = slice(BANK_PAIRS * h, BANK_PAIRS * (h + 1))
            nc.scalar.copy(out=result_of[t][:, pairs, :], in_=difference_of[(t, h)][:])
            store(t, h)

        def in_range(t):
            return 0 <= t < TILES

        flips_in = flips_by_step()
        for t in range(FIRST_STEP, TILES):
            if t == FIRST_STEP:
                early_fractions(list(range(HEAD_TILES)))
            late = t >= TILES - CHUNK
            if late and in_range(t + PROJECT_AHEAD):
                project(t + PROJECT_AHEAD)
            if in_range(t - 1) and tensor_subtracts(t - 1, 0):
                subtract_on_tensor(t - 1, 0)
            if in_range(t) and in_range(t + FRAC_AHEAD):
                whole_turns(t + FRAC_AHEAD)
            if in_range(t + TRIG_AHEAD):
                sine_and_versine(t + TRIG_AHEAD)
            for flipped_tile in flips_in.get(t, []):
                flip(flipped_tile)
            if in_range(t - 1) and tensor_subtracts(t - 1, 0):
                copy_difference_and_store(t - 1, 0)
            if in_range(t):
                rotate_and_store(t, 0)
            if t + PROJECT_AHEAD in CHUNK_FIRST:
                quantise(chunk_of[t + PROJECT_AHEAD])
            if t == FIRST_STEP + 1:
                early_fractions(list(range(HEAD_TILES, FRAC_AHEAD)))
                turns_to_columns()
                multiply_idly(IDLE_SECOND)
            if in_range(t + PROJECT_AHEAD) and not late:
                project(t + PROJECT_AHEAD)
            if t == FIRST_STEP + 1:
                columns_to_psum()
            if in_range(t):
                rotate_and_store(t, 1)
            if in_range(t) and in_range(t + FRAC_AHEAD):
                fraction(t + FRAC_AHEAD)
